import numpy as np
import ml_dtypes


def mxq(x, axis, fmt="e4m3"):
    dtype, down = {"e4m3": (ml_dtypes.float8_e4m3fn, 7), "e5m2": (ml_dtypes.float8_e5m2, 14)}[fmt]
    v = np.moveaxis(np.asarray(x, np.float32).astype(ml_dtypes.bfloat16).astype(np.float64), axis, -1)
    blocks = v.reshape(v.shape[:-1] + (-1, 32))
    amax = np.abs(blocks).max(-1, keepdims=True)
    byte = np.maximum(np.where(amax > 0, np.frexp(amax)[1] - 1 + 127, 0) - down, 1)
    scale = np.exp2(byte - 127.0)
    codes = (blocks / scale).astype(np.float32).astype(dtype).astype(np.float64)
    return np.moveaxis((codes * scale).reshape(v.shape), -1, axis)


WIDE = False


def mx_kscale(k):
    if not WIDE:
        return np.ones(k)
    levels = np.array([10, -10, 5, -5, 0])
    a = np.random.permutation(np.resize(levels, k // 512 * 4)).reshape(k // 512, 4)
    idx = np.arange(k)
    return np.exp2(a[idx // 512, idx % 128 // 32])


BF16 = ml_dtypes.bfloat16


def bf(x):
    return np.asarray(x, np.float32).astype(BF16)


def f64(x):
    return np.asarray(x).astype(np.float64)


D, KW, STRIDE, STACK, B, O = 32, 11, 3, 8, 128, 128
W_IN = D * D
POS = (D - KW) // STRIDE + 1
K = STACK * POS * POS


def build_mask():
    base_new = np.tile(np.arange(KW), KW)
    addition_new = np.repeat(np.arange(KW) * D, KW)
    index_1 = addition_new + base_new
    index_width = np.tile(index_1, POS)
    addition_width = np.repeat(STRIDE * np.arange(POS), KW * KW)
    index_row = index_width + addition_width
    index_column = np.tile(index_row, POS)
    addition_height = np.repeat(STRIDE * D * np.arange(POS), KW * KW * POS)
    index_final = index_column + addition_height
    stack = np.repeat(np.arange(POS * POS), KW * KW)
    block = np.zeros((POS * POS, W_IN))
    block[stack, index_final] = 1.0
    return np.vstack([block] * STACK)


def setup_inputs():
    s, t = mx_kscale(W_IN), mx_kscale(K)
    return {"z": bf(np.random.standard_normal((B, W_IN)) * s),
            "T3": bf(np.random.standard_normal((K, W_IN)) * 0.7 / np.sqrt(KW * KW) / s),
            "mask": bf(build_mask()),
            "x1": bf(np.random.standard_normal((B, K)) * 0.7 * t),
            "x2": bf(np.random.standard_normal((B, K)) * 1.4 * t),
            "C_w": bf(np.random.standard_normal((O, K)) / np.sqrt(K) / t),
            "C_b": bf(np.random.standard_normal(O) * 0.5)}


def reference(z, T3, mask, x1, x2, C_w, C_b):
    zq = mxq(f64(z).reshape(-1, D * D), 1, "e4m3")
    p3 = zq @ mxq(f64(mask) * f64(T3), 1, "e4m3").T
    x3 = 2.0 * p3 * f64(x2) - f64(x1)
    return (mxq(x3, 1, "e4m3") @ mxq(f64(C_w), 1, "e4m3").T) + f64(C_b)

@@ -1,0 +1,158 @@
+from contextlib import ExitStack
+
+import concourse.mybir as mybir
+from concourse.masks import make_identity
+
+F32 = mybir.dt.float32
+BF16 = mybir.dt.bfloat16
+U32 = mybir.dt.uint32
+U8 = mybir.dt.uint8
+FP8X4 = mybir.dt.float8_e4m3fn_x4
+MULT = mybir.AluOpType.mult
+SUBTRACT = mybir.AluOpType.subtract
+ADD = mybir.AluOpType.add
+
+P = 128
+PACK = 4
+K_PASS = P * PACK
+HALVES = 2
+
+B = 128
+W_IN = 1024
+K = 512
+O = 128
+PASSES_1 = W_IN // K_PASS
+ROW_TILES = K // P
+
+FLOPS = 2 * B * W_IN * K + 2 * B * K * O
+
+
+def transpose_words(nc, psum_tile, source, identity):
+    words = source.bitcast(F32)
+    for j in range(words.shape[1] // P):
+        nc.tensor.transpose(psum_tile[:, j, :], words[:, j * P : (j + 1) * P], identity)
+
+
+def grouped_view(grouped, passes):
+    return grouped.bitcast(F32).rearrange("q (c r u) -> q c r u", c=passes, u=HALVES)
+
+
+def tile_chebyshev_l3_sparsed32_stack_pb_s_kernel(tc, z, T3, mask, x1, x2, C_w, C_b, out):
+    nc = tc.nc
+    with ExitStack() as ctx:
+        keep = ctx.enter_context(tc.tile_pool(name="keep", bufs=1))
+        loads = ctx.enter_context(tc.tile_pool(name="loads", bufs=ROW_TILES))
+        work = ctx.enter_context(tc.tile_pool(name="work", bufs=2))
+        psum = ctx.enter_context(tc.psum_pool(name="psum", bufs=1))
+        psum_w = ctx.enter_context(tc.psum_pool(name="psum_w", bufs=2))
+
+        identity = keep.tile([P, P], F32)
+        make_identity(nc, identity[:])
+
+        z_sb = keep.tile([B, W_IN], BF16)
+        nc.sync.dma_start(out=z_sb[:], in_=z)
+        t3_tiles = []
+        mask_tiles = []
+        for t in range(ROW_TILES):
+            rows = slice(t * P, (t + 1) * P)
+            t3_sb = loads.tile([P, W_IN], BF16)
+            nc.sync.dma_start(out=t3_sb[:], in_=T3[rows, :])
+            mask_sb = loads.tile([P, W_IN], BF16)
+            nc.scalar.dma_start(out=mask_sb[:], in_=mask[rows, :])
+            t3_tiles.append(t3_sb)
+            mask_tiles.append(mask_sb)
+        x2_sb = keep.tile([B, K], BF16)
+        nc.sync.dma_start(out=x2_sb[:], in_=x2)
+        x1_sb = keep.tile([B, K], BF16)
+        nc.scalar.dma_start(out=x1_sb[:], in_=x1)
+        cw_sb = keep.tile([O, K], BF16)
+        nc.sync.dma_start(out=cw_sb[:], in_=C_w)
+        bias_sb = keep.tile([B, O], BF16)
+        nc.scalar.dma_start(out=bias_sb[:], in_=C_b.partition_broadcast(B))
+
+        zT_ps = psum.tile([P, PASSES_1 * HALVES, B], F32)
+        transpose_words(nc, zT_ps, z_sb[:], identity[:])
+        z_grouped = keep.tile([P, PASSES_1 * B * PACK], BF16, align_bytes=64)
+        nc.scalar.copy(
+            out=grouped_view(z_grouped[:], PASSES_1),
+            in_=zT_ps[:].rearrange("q (c u) r -> q c r u", u=HALVES),
+        )
+        z_codes = keep.tile([P, PASSES_1, B], U32, align_bytes=64)
+        z_scales = keep.tile([P, PASSES_1, B], U8, align_bytes=64)
+        nc.vector.quantize_mx(
+            out=z_codes[:].rearrange("q c r -> q (c r)").bitcast(FP8X4),
+            scales=z_scales[:].rearrange("q c r -> q (c r)"),
+            in_=z_grouped[:],
+        )
+
+        p3_ps = psum.tile([B, K], F32)
+        x3_sb = keep.tile([B, K], BF16)
+        for t in range(ROW_TILES):
+            cols = slice(t * P, (t + 1) * P)
+            masked = work.tile([P, W_IN], BF16)
+            nc.vector.tensor_tensor(out=masked[:], in0=t3_tiles[t][:], in1=mask_tiles[t][:], op=MULT)
+            wT_ps = psum_w.tile([P, PASSES_1 * HALVES, P], F32)
+            transpose_words(nc, wT_ps, masked[:], identity[:])
+            w_grouped = work.tile([P, PASSES_1 * P * PACK], BF16, align_bytes=64)
+            nc.scalar.copy(
+                out=grouped_view(w_grouped[:], PASSES_1),
+                in_=wT_ps[:].rearrange("q (c u) r -> q c r u", u=HALVES),
+            )
+            w_codes = work.tile([P, PASSES_1, P], U32, align_bytes=64)
+            w_scales = work.tile([P, PASSES_1, P], U8, align_bytes=64)
+            nc.vector.quantize_mx(
+                out=w_codes[:].rearrange("q c r -> q (c r)").bitcast(FP8X4),
+                scales=w_scales[:].rearrange("q c r -> q (c r)"),
+                in_=w_grouped[:],
+            )
+            for c in range(PASSES_1):
+                nc.tensor.matmul_mx(
+                    out=p3_ps[:, cols],
+                    lhsT=z_codes[:, c, :].bitcast(FP8X4),
+                    lhsT_scale=z_scales[:, c, :],
+                    rhs=w_codes[:, c, :].bitcast(FP8X4),
+                    rhs_scale=w_scales[:, c, :],
+                    start=(c == 0),
+                    stop=(c == PASSES_1 - 1),
+                )
+            doubled = work.tile([B, P], F32)
+            nc.vector.scalar_tensor_tensor(
+                out=doubled[:], in0=p3_ps[:, cols], scalar=2.0, in1=x2_sb[:, cols], op0=MULT, op1=MULT
+            )
+            nc.vector.tensor_tensor(out=x3_sb[:, cols], in0=doubled[:], in1=x1_sb[:, cols], op=SUBTRACT)
+
+        cwT_ps = psum.tile([P, HALVES, O], F32)
+        transpose_words(nc, cwT_ps, cw_sb[:], identity[:])
+        cw_grouped = keep.tile([P, O * PACK], BF16, align_bytes=64)
+        nc.scalar.copy(
+            out=grouped_view(cw_grouped[:], 1),
+            in_=cwT_ps[:].rearrange("q (c u) r -> q c r u", u=HALVES),
+        )
+        cw_codes = keep.tile([P, O], U32, align_bytes=64)
+        cw_scales = keep.tile([P, O], U8, align_bytes=64)
+        nc.vector.quantize_mx(out=cw_codes[:].bitcast(FP8X4), scales=cw_scales[:], in_=cw_grouped[:])
+
+        x3T_ps = psum.tile([P, HALVES, B], F32)
+        transpose_words(nc, x3T_ps, x3_sb[:], identity[:])
+        x3_grouped = keep.tile([P, B * PACK], BF16, align_bytes=64)
+        nc.vector.tensor_copy(
+            out=grouped_view(x3_grouped[:], 1),
+            in_=x3T_ps[:].rearrange("q (c u) r -> q c r u", u=HALVES),
+        )
+        x3_codes = keep.tile([P, B], U32, align_bytes=64)
+        x3_scales = keep.tile([P, B], U8, align_bytes=64)
+        nc.vector.quantize_mx(out=x3_codes[:].bitcast(FP8X4), scales=x3_scales[:], in_=x3_grouped[:])
+
+        out_ps = psum.tile([B, O], F32)
+        nc.tensor.matmul_mx(
+            out=out_ps[:],
+            lhsT=x3_codes[:].bitcast(FP8X4),
+            lhsT_scale=x3_scales[:],
+            rhs=cw_codes[:].bitcast(FP8X4),
+            rhs_scale=cw_scales[:],
+            start=True,
+            stop=True,
+        )
+        out_sb = keep.tile([B, O], F32)
+        nc.vector.tensor_tensor(out=out_sb[:], in0=out_ps[:], in1=bias_sb[:], op=ADD)
+        nc.sync.dma_start(out=out, in_=out_sb[:])

@@ -15,50 +15,65 @@ ADD = mybir.AluOpType.add
 P = 128
 PACK = 4
 K_PASS = P * PACK
-HALVES = 2
+PAIR = 2
+HALVES = PACK // PAIR
 
+D = 32
+KW = 11
+STRIDE = 3
+POS = 8
+STACK = 8
 B = 128
-W_IN = 1024
-K = 512
+K = STACK * POS * POS
 O = 128
-PASSES_1 = W_IN // K_PASS
-ROW_TILES = K // P
 
-FLOPS = 2 * B * W_IN * K + 2 * B * K * O
+GROUPS = K // P
+PATCH_ROWS = POS // GROUPS
+IN_GROUP = PATCH_ROWS * POS
+WINDOW_ROWS = K_PASS // D
+assert STRIDE * (PATCH_ROWS - 1) + KW <= WINDOW_ROWS
+
+FLOPS = 2 * B * D * D * K + 2 * B * K * O
 
 
-def transpose_words(nc, psum_tile, source, identity):
+def window_start(g):
+    return D * min(g * PATCH_ROWS * STRIDE, D - WINDOW_ROWS)
+
+
+def transpose_pass(nc, psum_view, source, identity):
     words = source.bitcast(F32)
-    for j in range(words.shape[1] // P):
-        nc.tensor.transpose(psum_tile[:, j, :], words[:, j * P : (j + 1) * P], identity)
+    for u in range(HALVES):
+        nc.tensor.transpose(psum_view[:, u, :], words[:, u : K_PASS // PAIR : HALVES], identity)
 
 
-def grouped_view(grouped, passes):
-    return grouped.bitcast(F32).rearrange("q (c r u) -> q c r u", c=passes, u=HALVES)
+def grouped_words(grouped):
+    return grouped.bitcast(F32).rearrange("q (r u) -> q r u", u=HALVES)
 
 
 def tile_chebyshev_l3_sparsed32_stack_pb_s_kernel(tc, z, T3, mask, x1, x2, C_w, C_b, out):
     nc = tc.nc
     with ExitStack() as ctx:
         keep = ctx.enter_context(tc.tile_pool(name="keep", bufs=1))
-        loads = ctx.enter_context(tc.tile_pool(name="loads", bufs=ROW_TILES))
+        loads = ctx.enter_context(tc.tile_pool(name="loads", bufs=GROUPS))
         work = ctx.enter_context(tc.tile_pool(name="work", bufs=2))
         psum = ctx.enter_context(tc.psum_pool(name="psum", bufs=1))
-        psum_w = ctx.enter_context(tc.psum_pool(name="psum_w", bufs=2))
+        psum_t = ctx.enter_context(tc.psum_pool(name="psum_t", bufs=2))
 
         identity = keep.tile([P, P], F32)
         make_identity(nc, identity[:])
 
-        z_sb = keep.tile([B, W_IN], BF16)
+        z_sb = keep.tile([B, D * D], BF16)
         nc.sync.dma_start(out=z_sb[:], in_=z)
+        t3_groups = T3.rearrange("(s g c) w -> g c s w", s=STACK, g=GROUPS)
+        mask_groups = mask.rearrange("(s g c) w -> g c s w", s=STACK, g=GROUPS)
         t3_tiles = []
         mask_tiles = []
-        for t in range(ROW_TILES):
-            rows = slice(t * P, (t + 1) * P)
-            t3_sb = loads.tile([P, W_IN], BF16)
-            nc.sync.dma_start(out=t3_sb[:], in_=T3[rows, :])
-            mask_sb = loads.tile([P, W_IN], BF16)
-            nc.scalar.dma_start(out=mask_sb[:], in_=mask[rows, :])
+        for g in range(GROUPS):
+            window = slice(window_start(g), window_start(g) + K_PASS)
+            t3_sb = loads.tile([P, K_PASS], BF16)
+            nc.sync.dma_start(out=t3_sb[:], in_=t3_groups[g, :, :, window])
+            mask_sb = loads.tile([P, K_PASS], BF16)
+            nc.scalar.dma_start(out=mask_sb[:], in_=mask_groups[g, :, :, window])
             t3_tiles.append(t3_sb)
             mask_tiles.append(mask_sb)
         x2_sb = keep.tile([B, K], BF16)
@@ -70,75 +85,64 @@ def tile_chebyshev_l3_sparsed32_stack_pb_s_kernel(tc, z, T3, mask, x1, x2, C_w, 
         bias_sb = keep.tile([B, O], BF16)
         nc.scalar.dma_start(out=bias_sb[:], in_=C_b.partition_broadcast(B))
 
-        zT_ps = psum.tile([P, PASSES_1 * HALVES, B], F32)
-        transpose_words(nc, zT_ps, z_sb[:], identity[:])
-        z_grouped = keep.tile([P, PASSES_1 * B * PACK], BF16, align_bytes=64)
-        nc.scalar.copy(
-            out=grouped_view(z_grouped[:], PASSES_1),
-            in_=zT_ps[:].rearrange("q (c u) r -> q c r u", u=HALVES),
-        )
-        z_codes = keep.tile([P, PASSES_1, B], U32, align_bytes=64)
-        z_scales = keep.tile([P, PASSES_1, B], U8, align_bytes=64)
-        nc.vector.quantize_mx(
-            out=z_codes[:].rearrange("q c r -> q (c r)").bitcast(FP8X4),
-            scales=z_scales[:].rearrange("q c r -> q (c r)"),
-            in_=z_grouped[:],
-        )
-
-        p3_ps = psum.tile([B, K], F32)
-        x3_sb = keep.tile([B, K], BF16)
-        for t in range(ROW_TILES):
-            cols = slice(t * P, (t + 1) * P)
-            masked = work.tile([P, W_IN], BF16)
-            nc.vector.tensor_tensor(out=masked[:], in0=t3_tiles[t][:], in1=mask_tiles[t][:], op=MULT)
-            wT_ps = psum_w.tile([P, PASSES_1 * HALVES, P], F32)
-            transpose_words(nc, wT_ps, masked[:], identity[:])
-            w_grouped = work.tile([P, PASSES_1 * P * PACK], BF16, align_bytes=64)
-            nc.scalar.copy(
-                out=grouped_view(w_grouped[:], PASSES_1),
-                in_=wT_ps[:].rearrange("q (c u) r -> q c r u", u=HALVES),
-            )
-            w_codes = work.tile([P, PASSES_1, P], U32, align_bytes=64)
-            w_scales = work.tile([P, PASSES_1, P], U8, align_bytes=64)
+        z_codes = keep.tile([P, GROUPS, B], U32, align_bytes=64)
+        z_scales = keep.tile([P, GROUPS, B], U8, align_bytes=64)
+        for g in range(GROUPS):
+            zT_ps = psum_t.tile([P, HALVES, B], F32)
+            transpose_pass(nc, zT_ps, z_sb[:, window_start(g) : window_start(g) + K_PASS], identity[:])
+            z_grouped = work.tile([P, B * PACK], BF16, align_bytes=64)
+            nc.scalar.copy(out=grouped_words(z_grouped[:]), in_=zT_ps[:].rearrange("q u r -> q r u"))
             nc.vector.quantize_mx(
-                out=w_codes[:].rearrange("q c r -> q (c r)").bitcast(FP8X4),
-                scales=w_scales[:].rearrange("q c r -> q (c r)"),
-                in_=w_grouped[:],
+                out=z_codes[:, g, :].bitcast(FP8X4), scales=z_scales[:, g, :], in_=z_grouped[:]
             )
-            for c in range(PASSES_1):
-                nc.tensor.matmul_mx(
-                    out=p3_ps[:, cols],
-                    lhsT=z_codes[:, c, :].bitcast(FP8X4),
-                    lhsT_scale=z_scales[:, c, :],
-                    rhs=w_codes[:, c, :].bitcast(FP8X4),
-                    rhs_scale=w_scales[:, c, :],
-                    start=(c == 0),
-                    stop=(c == PASSES_1 - 1),
-                )
-            doubled = work.tile([B, P], F32)
+
+        p3_ps = psum.tile([B, GROUPS, IN_GROUP, STACK], F32)
+        x3_sb = keep.tile([B, K], BF16)
+        x1_by_group = x1_sb[:].rearrange("b (s g c) -> b g s c", s=STACK, g=GROUPS)
+        x2_by_group = x2_sb[:].rearrange("b (s g c) -> b g s c", s=STACK, g=GROUPS)
+        x3_by_group = x3_sb[:].rearrange("b (s g c) -> b g s c", s=STACK, g=GROUPS)
+        for g in range(GROUPS):
+            masked = work.tile([P, K_PASS], BF16)
+            nc.vector.tensor_tensor(out=masked[:], in0=t3_tiles[g][:], in1=mask_tiles[g][:], op=MULT)
+            wT_ps = psum_t.tile([P, HALVES, P], F32)
+            transpose_pass(nc, wT_ps, masked[:], identity[:])
+            w_grouped = work.tile([P, P * PACK], BF16, align_bytes=64)
+            nc.scalar.copy(out=grouped_words(w_grouped[:]), in_=wT_ps[:].rearrange("q u r -> q r u"))
+            w_codes = work.tile([P, P], U32, align_bytes=64)
+            w_scales = work.tile([P, P], U8, align_bytes=64)
+            nc.vector.quantize_mx(out=w_codes[:].bitcast(FP8X4), scales=w_scales[:], in_=w_grouped[:])
+            nc.tensor.matmul_mx(
+                out=p3_ps[:, g].rearrange("b c s -> b (c s)"),
+                lhsT=z_codes[:, g, :].bitcast(FP8X4),
+                lhsT_scale=z_scales[:, g, :],
+                rhs=w_codes[:].bitcast(FP8X4),
+                rhs_scale=w_scales[:],
+                start=True,
+                stop=True,
+            )
+            doubled = work.tile([B, STACK, IN_GROUP], F32)
             nc.vector.scalar_tensor_tensor(
-                out=doubled[:], in0=p3_ps[:, cols], scalar=2.0, in1=x2_sb[:, cols], op0=MULT, op1=MULT
+                out=doubled[:],
+                in0=p3_ps[:, g].rearrange("b c s -> b s c"),
+                scalar=2.0,
+                in1=x2_by_group[:, g],
+                op0=MULT,
+                op1=MULT,
             )
-            nc.vector.tensor_tensor(out=x3_sb[:, cols], in0=doubled[:], in1=x1_sb[:, cols], op=SUBTRACT)
+            nc.vector.tensor_tensor(out=x3_by_group[:, g], in0=doubled[:], in1=x1_by_group[:, g], op=SUBTRACT)
 
         cwT_ps = psum.tile([P, HALVES, O], F32)
-        transpose_words(nc, cwT_ps, cw_sb[:], identity[:])
+        transpose_pass(nc, cwT_ps, cw_sb[:], identity[:])
         cw_grouped = keep.tile([P, O * PACK], BF16, align_bytes=64)
-        nc.scalar.copy(
-            out=grouped_view(cw_grouped[:], 1),
-            in_=cwT_ps[:].rearrange("q (c u) r -> q c r u", u=HALVES),
-        )
+        nc.scalar.copy(out=grouped_words(cw_grouped[:]), in_=cwT_ps[:].rearrange("q u r -> q r u"))
         cw_codes = keep.tile([P, O], U32, align_bytes=64)
         cw_scales = keep.tile([P, O], U8, align_bytes=64)
         nc.vector.quantize_mx(out=cw_codes[:].bitcast(FP8X4), scales=cw_scales[:], in_=cw_grouped[:])
 
         x3T_ps = psum.tile([P, HALVES, B], F32)
-        transpose_words(nc, x3T_ps, x3_sb[:], identity[:])
+        transpose_pass(nc, x3T_ps, x3_sb[:], identity[:])
         x3_grouped = keep.tile([P, B * PACK], BF16, align_bytes=64)
-        nc.vector.tensor_copy(
-            out=grouped_view(x3_grouped[:], 1),
-            in_=x3T_ps[:].rearrange("q (c u) r -> q c r u", u=HALVES),
-        )
+        nc.vector.tensor_copy(out=grouped_words(x3_grouped[:]), in_=x3T_ps[:].rearrange("q u r -> q r u"))
         x3_codes = keep.tile([P, B], U32, align_bytes=64)
         x3_scales = keep.tile([P, B], U8, align_bytes=64)
         nc.vector.quantize_mx(out=x3_codes[:].bitcast(FP8X4), scales=x3_scales[:], in_=x3_grouped[:])

@@ -55,9 +55,9 @@ def tile_chebyshev_l3_sparsed32_stack_pb_s_kernel(tc, z, T3, mask, x1, x2, C_w, 
     with ExitStack() as ctx:
         keep = ctx.enter_context(tc.tile_pool(name="keep", bufs=1))
         loads = ctx.enter_context(tc.tile_pool(name="loads", bufs=GROUPS))
-        work = ctx.enter_context(tc.tile_pool(name="work", bufs=2))
+        work = ctx.enter_context(tc.tile_pool(name="work", bufs=GROUPS))
         psum = ctx.enter_context(tc.psum_pool(name="psum", bufs=1))
-        psum_t = ctx.enter_context(tc.psum_pool(name="psum_t", bufs=2))
+        psum_t = ctx.enter_context(tc.psum_pool(name="psum_t", bufs=6))
 
         identity = keep.tile([P, P], F32)
         make_identity(nc, identity[:])
@@ -73,25 +73,28 @@ def tile_chebyshev_l3_sparsed32_stack_pb_s_kernel(tc, z, T3, mask, x1, x2, C_w, 
             t3_sb = loads.tile([P, K_PASS], BF16)
             nc.sync.dma_start(out=t3_sb[:], in_=t3_groups[g, :, :, window])
             mask_sb = loads.tile([P, K_PASS], BF16)
-            nc.scalar.dma_start(out=mask_sb[:], in_=mask_groups[g, :, :, window])
+            nc.sync.dma_start(out=mask_sb[:], in_=mask_groups[g, :, :, window])
             t3_tiles.append(t3_sb)
             mask_tiles.append(mask_sb)
         x2_sb = keep.tile([B, K], BF16)
         nc.sync.dma_start(out=x2_sb[:], in_=x2)
         x1_sb = keep.tile([B, K], BF16)
-        nc.scalar.dma_start(out=x1_sb[:], in_=x1)
+        nc.sync.dma_start(out=x1_sb[:], in_=x1)
         cw_sb = keep.tile([O, K], BF16)
         nc.sync.dma_start(out=cw_sb[:], in_=C_w)
         bias_sb = keep.tile([B, O], BF16)
-        nc.scalar.dma_start(out=bias_sb[:], in_=C_b.partition_broadcast(B))
+        nc.sync.dma_start(out=bias_sb[:], in_=C_b.partition_broadcast(B))
 
         z_codes = keep.tile([P, GROUPS, B], U32, align_bytes=64)
         z_scales = keep.tile([P, GROUPS, B], U8, align_bytes=64)
         for g in range(GROUPS):
-            zT_ps = psum_t.tile([P, HALVES, B], F32)
+            zT_ps = psum_t.tile([P, HALVES, B], F32, tag="transposed")
             transpose_pass(nc, zT_ps, z_sb[:, window_start(g) : window_start(g) + K_PASS], identity[:])
             z_grouped = work.tile([P, B * PACK], BF16, align_bytes=64)
-            nc.scalar.copy(out=grouped_words(z_grouped[:]), in_=zT_ps[:].rearrange("q u r -> q r u"))
+            if g % 2 == 0:
+                nc.scalar.copy(out=grouped_words(z_grouped[:]), in_=zT_ps[:].rearrange("q u r -> q r u"))
+            else:
+                nc.vector.tensor_copy(out=grouped_words(z_grouped[:]), in_=zT_ps[:].rearrange("q u r -> q r u"))
             nc.vector.quantize_mx(
                 out=z_codes[:, g, :].bitcast(FP8X4), scales=z_scales[:, g, :], in_=z_grouped[:]
             )
@@ -104,7 +107,7 @@ def tile_chebyshev_l3_sparsed32_stack_pb_s_kernel(tc, z, T3, mask, x1, x2, C_w, 
         for g in range(GROUPS):
             masked = work.tile([P, K_PASS], BF16)
             nc.vector.tensor_tensor(out=masked[:], in0=t3_tiles[g][:], in1=mask_tiles[g][:], op=MULT)
-            wT_ps = psum_t.tile([P, HALVES, P], F32)
+            wT_ps = psum_t.tile([P, HALVES, P], F32, tag="transposed")
             transpose_pass(nc, wT_ps, masked[:], identity[:])
             w_grouped = work.tile([P, P * PACK], BF16, align_bytes=64)
             nc.scalar.copy(out=grouped_words(w_grouped[:]), in_=wT_ps[:].rearrange("q u r -> q r u"))
@@ -131,7 +134,7 @@ def tile_chebyshev_l3_sparsed32_stack_pb_s_kernel(tc, z, T3, mask, x1, x2, C_w, 
             )
             nc.vector.tensor_tensor(out=x3_by_group[:, g], in0=doubled[:], in1=x1_by_group[:, g], op=SUBTRACT)
 
-        cwT_ps = psum.tile([P, HALVES, O], F32)
+        cwT_ps = psum_t.tile([P, HALVES, O], F32, tag="transposed")
         transpose_pass(nc, cwT_ps, cw_sb[:], identity[:])
         cw_grouped = keep.tile([P, O * PACK], BF16, align_bytes=64)
         nc.scalar.copy(out=grouped_words(cw_grouped[:]), in_=cwT_ps[:].rearrange("q u r -> q r u"))
@@ -139,7 +142,7 @@ def tile_chebyshev_l3_sparsed32_stack_pb_s_kernel(tc, z, T3, mask, x1, x2, C_w, 
         cw_scales = keep.tile([P, O], U8, align_bytes=64)
         nc.vector.quantize_mx(out=cw_codes[:].bitcast(FP8X4), scales=cw_scales[:], in_=cw_grouped[:])
 
-        x3T_ps = psum.tile([P, HALVES, B], F32)
+        x3T_ps = psum_t.tile([P, HALVES, B], F32, tag="transposed")
         transpose_pass(nc, x3T_ps, x3_sb[:], identity[:])
         x3_grouped = keep.tile([P, B * PACK], BF16, align_bytes=64)
         nc.vector.tensor_copy(out=grouped_words(x3_grouped[:]), in_=x3T_ps[:].rearrange("q u r -> q r u"))

@@ -40,10 +40,14 @@ def window_start(g):
     return D * min(g * PATCH_ROWS * STRIDE, D - WINDOW_ROWS)
 
 
-def transpose_pass(nc, psum_view, source, identity):
+def every_second_word(source):
     words = source.bitcast(F32)
+    return [words[:, u : K_PASS // PAIR : HALVES] for u in range(HALVES)]
+
+
+def transpose_pass(nc, psum_view, word_blocks, identity):
     for u in range(HALVES):
-        nc.tensor.transpose(psum_view[:, u, :], words[:, u : K_PASS // PAIR : HALVES], identity)
+        nc.tensor.transpose(psum_view[:, u, :], word_blocks[u], identity)
 
 
 def grouped_words(grouped):
@@ -57,7 +61,8 @@ def tile_chebyshev_l3_sparsed32_stack_pb_s_kernel(tc, z, T3, mask, x1, x2, C_w, 
         loads = ctx.enter_context(tc.tile_pool(name="loads", bufs=GROUPS))
         work = ctx.enter_context(tc.tile_pool(name="work", bufs=GROUPS))
         psum = ctx.enter_context(tc.psum_pool(name="psum", bufs=1))
-        psum_t = ctx.enter_context(tc.psum_pool(name="psum_t", bufs=6))
+        psum_p3 = ctx.enter_context(tc.psum_pool(name="psum_p3", bufs=2))
+        psum_t = ctx.enter_context(tc.psum_pool(name="psum_t", bufs=5))
 
         identity = keep.tile([P, P], F32)
         make_identity(nc, identity[:])
@@ -89,7 +94,8 @@ def tile_chebyshev_l3_sparsed32_stack_pb_s_kernel(tc, z, T3, mask, x1, x2, C_w, 
         z_scales = keep.tile([P, GROUPS, B], U8, align_bytes=64)
         for g in range(GROUPS):
             zT_ps = psum_t.tile([P, HALVES, B], F32, tag="transposed")
-            transpose_pass(nc, zT_ps, z_sb[:, window_start(g) : window_start(g) + K_PASS], identity[:])
+            window = slice(window_start(g), window_start(g) + K_PASS)
+            transpose_pass(nc, zT_ps, every_second_word(z_sb[:, window]), identity[:])
             z_grouped = work.tile([P, B * PACK], BF16, align_bytes=64)
             if g % 2 == 0:
                 nc.scalar.copy(out=grouped_words(z_grouped[:]), in_=zT_ps[:].rearrange("q u r -> q r u"))
@@ -99,23 +105,29 @@ def tile_chebyshev_l3_sparsed32_stack_pb_s_kernel(tc, z, T3, mask, x1, x2, C_w, 
                 out=z_codes[:, g, :].bitcast(FP8X4), scales=z_scales[:, g, :], in_=z_grouped[:]
             )
 
-        p3_ps = psum.tile([B, GROUPS, IN_GROUP, STACK], F32)
         x3_sb = keep.tile([B, K], BF16)
         x1_by_group = x1_sb[:].rearrange("b (s g c) -> b g s c", s=STACK, g=GROUPS)
         x2_by_group = x2_sb[:].rearrange("b (s g c) -> b g s c", s=STACK, g=GROUPS)
         x3_by_group = x3_sb[:].rearrange("b (s g c) -> b g s c", s=STACK, g=GROUPS)
         for g in range(GROUPS):
-            masked = work.tile([P, K_PASS], BF16)
-            nc.vector.tensor_tensor(out=masked[:], in0=t3_tiles[g][:], in1=mask_tiles[g][:], op=MULT)
+            masked = work.tile([P, HALVES, P, PAIR], BF16)
+            nc.vector.tensor_tensor(
+                out=masked[:],
+                in0=t3_tiles[g][:].rearrange("r (q u e) -> r u q e", u=HALVES, e=PAIR),
+                in1=mask_tiles[g][:].rearrange("r (q u e) -> r u q e", u=HALVES, e=PAIR),
+                op=MULT,
+            )
+            masked_words = masked[:].rearrange("r u q e -> r (u q e)").bitcast(F32)
             wT_ps = psum_t.tile([P, HALVES, P], F32, tag="transposed")
-            transpose_pass(nc, wT_ps, masked[:], identity[:])
+            transpose_pass(nc, wT_ps, [masked_words[:, u * P : (u + 1) * P] for u in range(HALVES)], identity[:])
             w_grouped = work.tile([P, P * PACK], BF16, align_bytes=64)
             nc.scalar.copy(out=grouped_words(w_grouped[:]), in_=wT_ps[:].rearrange("q u r -> q r u"))
             w_codes = work.tile([P, P], U32, align_bytes=64)
             w_scales = work.tile([P, P], U8, align_bytes=64)
             nc.vector.quantize_mx(out=w_codes[:].bitcast(FP8X4), scales=w_scales[:], in_=w_grouped[:])
+            p3_ps = psum_p3.tile([B, IN_GROUP, STACK], F32)
             nc.tensor.matmul_mx(
-                out=p3_ps[:, g].rearrange("b c s -> b (c s)"),
+                out=p3_ps[:].rearrange("b c s -> b (c s)"),
                 lhsT=z_codes[:, g, :].bitcast(FP8X4),
                 lhsT_scale=z_scales[:, g, :],
                 rhs=w_codes[:].bitcast(FP8X4),
@@ -126,7 +138,7 @@ def tile_chebyshev_l3_sparsed32_stack_pb_s_kernel(tc, z, T3, mask, x1, x2, C_w, 
             doubled = work.tile([B, STACK, IN_GROUP], F32)
             nc.vector.scalar_tensor_tensor(
                 out=doubled[:],
-                in0=p3_ps[:, g].rearrange("b c s -> b s c"),
+                in0=p3_ps[:].rearrange("b c s -> b s c"),
                 scalar=2.0,
                 in1=x2_by_group[:, g],
                 op0=MULT,
@@ -135,7 +147,7 @@ def tile_chebyshev_l3_sparsed32_stack_pb_s_kernel(tc, z, T3, mask, x1, x2, C_w, 
             nc.vector.tensor_tensor(out=x3_by_group[:, g], in0=doubled[:], in1=x1_by_group[:, g], op=SUBTRACT)
 
         cwT_ps = psum_t.tile([P, HALVES, O], F32, tag="transposed")
-        transpose_pass(nc, cwT_ps, cw_sb[:], identity[:])
+        transpose_pass(nc, cwT_ps, every_second_word(cw_sb[:]), identity[:])
         cw_grouped = keep.tile([P, O * PACK], BF16, align_bytes=64)
         nc.scalar.copy(out=grouped_words(cw_grouped[:]), in_=cwT_ps[:].rearrange("q u r -> q r u"))
         cw_codes = keep.tile([P, O], U32, align_bytes=64)
@@ -143,7 +155,7 @@ def tile_chebyshev_l3_sparsed32_stack_pb_s_kernel(tc, z, T3, mask, x1, x2, C_w, 
         nc.vector.quantize_mx(out=cw_codes[:].bitcast(FP8X4), scales=cw_scales[:], in_=cw_grouped[:])
 
         x3T_ps = psum_t.tile([P, HALVES, B], F32, tag="transposed")
-        transpose_pass(nc, x3T_ps, x3_sb[:], identity[:])
+        transpose_pass(nc, x3T_ps, every_second_word(x3_sb[:]), identity[:])
         x3_grouped = keep.tile([P, B * PACK], BF16, align_bytes=64)
         nc.vector.tensor_copy(out=grouped_words(x3_grouped[:]), in_=x3T_ps[:].rearrange("q u r -> q r u"))
         x3_codes = keep.tile([P, B], U32, align_bytes=64)

@@ -7,6 +7,7 @@ F32 = mybir.dt.float32
 BF16 = mybir.dt.bfloat16
 U32 = mybir.dt.uint32
 U8 = mybir.dt.uint8
+I32 = mybir.dt.int32
 FP8X4 = mybir.dt.float8_e4m3fn_x4
 MULT = mybir.AluOpType.mult
 SUBTRACT = mybir.AluOpType.subtract
@@ -54,6 +55,13 @@ def grouped_words(grouped):
     return grouped.bitcast(F32).rearrange("q (r u) -> q r u", u=HALVES)
 
 
+HALF = P // 2
+SLOTS = PACK
+ORDER = (0, 2, 1, 3)
+WAVES = 2
+WARM_PASSES = 8
+
+
 def tile_chebyshev_l3_sparsed32_stack_pb_s_kernel(tc, z, T3, mask, x1, x2, C_w, C_b, out):
     nc = tc.nc
     with ExitStack() as ctx:
@@ -61,26 +69,57 @@ def tile_chebyshev_l3_sparsed32_stack_pb_s_kernel(tc, z, T3, mask, x1, x2, C_w, 
         loads = ctx.enter_context(tc.tile_pool(name="loads", bufs=GROUPS))
         work = ctx.enter_context(tc.tile_pool(name="work", bufs=GROUPS))
         psum = ctx.enter_context(tc.psum_pool(name="psum", bufs=1))
-        psum_p3 = ctx.enter_context(tc.psum_pool(name="psum_p3", bufs=2))
-        psum_t = ctx.enter_context(tc.psum_pool(name="psum_t", bufs=5))
+        psum_x = ctx.enter_context(tc.psum_pool(name="psum_x", bufs=2))
+        psum_t = ctx.enter_context(tc.psum_pool(name="psum_t", bufs=4))
+
+        idle_grouped = keep.tile([P, P * PACK], BF16, align_bytes=64)
+        nc.vector.memset(idle_grouped[:].bitcast(F32), 0.0)
+        idle_codes = keep.tile([P, P], U32, align_bytes=64)
+        idle_scales = keep.tile([P, P], U8, align_bytes=64)
+        nc.vector.quantize_mx(out=idle_codes[:].bitcast(FP8X4), scales=idle_scales[:], in_=idle_grouped[:])
+        idle_ps = psum.tile([P, P], F32)
+        for n in range(WARM_PASSES):
+            nc.tensor.matmul_mx(
+                out=idle_ps[:],
+                lhsT=idle_codes[:].bitcast(FP8X4),
+                lhsT_scale=idle_scales[:],
+                rhs=idle_codes[:].bitcast(FP8X4),
+                rhs_scale=idle_scales[:],
+                start=True,
+                stop=True,
+            )
 
         identity = keep.tile([P, P], F32)
         make_identity(nc, identity[:])
+        swap = keep.tile([P, P], F32)
+        nc.gpsimd.tensor_copy(
+            out=swap[:].rearrange("r (a s j) -> r a s j", a=PATCH_ROWS, s=STACK),
+            in_=identity[:].rearrange("r (a j s) -> r a s j", a=PATCH_ROWS, s=STACK),
+        )
+        identity_bf = keep.tile([P, P], BF16)
+        make_identity(nc, identity_bf[:])
 
-        z_sb = keep.tile([B, D * D], BF16)
-        nc.sync.dma_start(out=z_sb[:], in_=z)
-        t3_groups = T3.rearrange("(s g c) w -> g c s w", s=STACK, g=GROUPS)
-        mask_groups = mask.rearrange("(s g c) w -> g c s w", s=STACK, g=GROUPS)
-        t3_tiles = []
-        mask_tiles = []
+        mask_sb = keep.tile([P, K_PASS], BF16)
+        nc.vector.memset(mask_sb[GROUPS * IN_GROUP :, :].bitcast(F32), 0.0)
         for g in range(GROUPS):
+            window = slice(window_start(g), window_start(g) + K_PASS)
+            rows = slice(g * IN_GROUP, (g + 1) * IN_GROUP)
+            nc.sync.dma_start(out=mask_sb[rows, :], in_=mask[rows, window])
+        t3_groups = T3.rearrange("(s g c) w -> g c s w", s=STACK, g=GROUPS)
+        t3_tiles = {}
+        z_sb = keep.tile([B, D * D], BF16)
+
+        def load_group(g):
             window = slice(window_start(g), window_start(g) + K_PASS)
             t3_sb = loads.tile([P, K_PASS], BF16)
             nc.sync.dma_start(out=t3_sb[:], in_=t3_groups[g, :, :, window])
-            mask_sb = loads.tile([P, K_PASS], BF16)
-            nc.sync.dma_start(out=mask_sb[:], in_=mask_groups[g, :, :, window])
-            t3_tiles.append(t3_sb)
-            mask_tiles.append(mask_sb)
+            t3_tiles[g] = t3_sb
+
+        load_group(ORDER[0])
+        nc.sync.dma_start(out=z_sb[:], in_=z)
+        load_group(ORDER[1])
+        load_group(ORDER[2])
+        load_group(ORDER[3])
         x2_sb = keep.tile([B, K], BF16)
         nc.sync.dma_start(out=x2_sb[:], in_=x2)
         x1_sb = keep.tile([B, K], BF16)
@@ -90,79 +129,168 @@ def tile_chebyshev_l3_sparsed32_stack_pb_s_kernel(tc, z, T3, mask, x1, x2, C_w, 
         bias_sb = keep.tile([B, O], BF16)
         nc.sync.dma_start(out=bias_sb[:], in_=C_b.partition_broadcast(B))
 
+        code_tiles = {}
+        for g in ORDER:
+            w_codes = work.tile([P, PATCH_ROWS, 2, HALF], U32, align_bytes=64)
+            w_scales = work.tile([P, PATCH_ROWS, 2, HALF], U8, align_bytes=64)
+            nc.vector.memset(w_codes[:, :, 1 - g // 2, :].bitcast(I32), 0)
+            nc.vector.memset(w_scales[:].rearrange("q a h m -> q (a h m)").bitcast(I32), 0)
+            code_tiles[g] = (w_codes, w_scales)
+
+        z_split = keep.tile([B, HALVES, D * D // PACK], F32)
+        z_grouped = keep.tile([P, GROUPS, B * PACK], BF16, align_bytes=64)
         z_codes = keep.tile([P, GROUPS, B], U32, align_bytes=64)
         z_scales = keep.tile([P, GROUPS, B], U8, align_bytes=64)
-        for g in range(GROUPS):
-            zT_ps = psum_t.tile([P, HALVES, B], F32, tag="transposed")
-            window = slice(window_start(g), window_start(g) + K_PASS)
-            transpose_pass(nc, zT_ps, every_second_word(z_sb[:, window]), identity[:])
-            z_grouped = work.tile([P, B * PACK], BF16, align_bytes=64)
-            if g % 2 == 0:
-                nc.scalar.copy(out=grouped_words(z_grouped[:]), in_=zT_ps[:].rearrange("q u r -> q r u"))
-            else:
-                nc.vector.tensor_copy(out=grouped_words(z_grouped[:]), in_=zT_ps[:].rearrange("q u r -> q r u"))
-            nc.vector.quantize_mx(
-                out=z_codes[:, g, :].bitcast(FP8X4), scales=z_scales[:, g, :], in_=z_grouped[:]
-            )
+        mask_t = keep.tile([P, GROUPS * IN_GROUP * PACK], BF16)
+        mask_by_group = mask_t[:].rearrange("q (g a j u e) -> q g a j u e", g=GROUPS, a=PATCH_ROWS, u=HALVES, e=PAIR)
+        x3_grouped = keep.tile([P, B * PACK], BF16, align_bytes=64)
+        x3_by_slot = x3_grouped[:].rearrange("p (b t) -> p b t", t=SLOTS)
+        x2_t = keep.tile([P, SLOTS, B], BF16)
+        x1_ps = psum.tile([P, SLOTS, B], BF16)
+        doubled = keep.tile([P, SLOTS, B], F32)
+        state = {}
 
-        x3_sb = keep.tile([B, K], BF16)
-        x1_by_group = x1_sb[:].rearrange("b (s g c) -> b g s c", s=STACK, g=GROUPS)
-        x2_by_group = x2_sb[:].rearrange("b (s g c) -> b g s c", s=STACK, g=GROUPS)
-        x3_by_group = x3_sb[:].rearrange("b (s g c) -> b g s c", s=STACK, g=GROUPS)
-        for g in range(GROUPS):
-            masked = work.tile([P, HALVES, P, PAIR], BF16)
+        def turn_weight(n):
+            wT_ps = psum_t.tile([P, HALVES, P], F32, tag="transposed")
+            transpose_pass(nc, wT_ps, every_second_word(t3_tiles[ORDER[n]][:]), swap[:])
+            state["wT", n] = wT_ps
+
+        def turn_z(n):
+            zT_ps = psum_t.tile([P, HALVES, B], F32, tag="transposed")
+            first = window_start(ORDER[n]) // PACK
+            transpose_pass(nc, zT_ps, [z_split[:, u, first : first + P] for u in range(HALVES)], identity[:])
+            nc.scalar.copy(out=grouped_words(z_grouped[:, n, :]), in_=zT_ps[:].rearrange("q u r -> q r u"))
+
+        def multiply_by_mask(n):
+            g = ORDER[n]
+            w_grouped = work.tile([P, P * PACK], BF16, align_bytes=64)
+            shape = [P, PATCH_ROWS, STACK, POS, HALVES, PAIR]
             nc.vector.tensor_tensor(
-                out=masked[:],
-                in0=t3_tiles[g][:].rearrange("r (q u e) -> r u q e", u=HALVES, e=PAIR),
-                in1=mask_tiles[g][:].rearrange("r (q u e) -> r u q e", u=HALVES, e=PAIR),
+                out=w_grouped[:].rearrange("q (a s j u e) -> q a s j u e", a=PATCH_ROWS, s=STACK, u=HALVES, e=PAIR),
+                in0=state["wT", n][:].bitcast(BF16).rearrange("q u (a s j e) -> q a s j u e", a=PATCH_ROWS, s=STACK, e=PAIR),
+                in1=mask_by_group[:, g].unsqueeze(2).to_broadcast(shape),
                 op=MULT,
             )
-            masked_words = masked[:].rearrange("r u q e -> r (u q e)").bitcast(F32)
-            wT_ps = psum_t.tile([P, HALVES, P], F32, tag="transposed")
-            transpose_pass(nc, wT_ps, [masked_words[:, u * P : (u + 1) * P] for u in range(HALVES)], identity[:])
-            w_grouped = work.tile([P, P * PACK], BF16, align_bytes=64)
-            nc.scalar.copy(out=grouped_words(w_grouped[:]), in_=wT_ps[:].rearrange("q u r -> q r u"))
-            w_codes = work.tile([P, P], U32, align_bytes=64)
-            w_scales = work.tile([P, P], U8, align_bytes=64)
-            nc.vector.quantize_mx(out=w_codes[:].bitcast(FP8X4), scales=w_scales[:], in_=w_grouped[:])
-            p3_ps = psum_p3.tile([B, IN_GROUP, STACK], F32)
-            nc.tensor.matmul_mx(
-                out=p3_ps[:].rearrange("b c s -> b (c s)"),
-                lhsT=z_codes[:, g, :].bitcast(FP8X4),
-                lhsT_scale=z_scales[:, g, :],
-                rhs=w_codes[:].bitcast(FP8X4),
-                rhs_scale=w_scales[:],
-                start=True,
-                stop=True,
+            state["w", n] = w_grouped
+
+        def quantize_weight(n):
+            g = ORDER[n]
+            w_codes, w_scales = code_tiles[g]
+            for a in range(PATCH_ROWS):
+                nc.vector.quantize_mx(
+                    out=w_codes[:, a, g // 2, :].bitcast(FP8X4),
+                    scales=w_scales[:, a, g // 2, :],
+                    in_=state["w", n][:, a * HALF * PACK : (a + 1) * HALF * PACK],
+                )
+
+        def quantize_z(w):
+            pair = slice(WAVES * w, WAVES * (w + 1))
+            nc.vector.quantize_mx(
+                out=z_codes[:, pair, :].rearrange("q n b -> q (n b)").bitcast(FP8X4),
+                scales=z_scales[:, pair, :].rearrange("q n b -> q (n b)"),
+                in_=z_grouped[:, pair, :].rearrange("q n x -> q (n x)"),
             )
-            doubled = work.tile([B, STACK, IN_GROUP], F32)
+
+        def first_product(w):
+            p3_ps = psum_x.tile([P, PATCH_ROWS, B], F32, tag="sums")
+            for a in range(PATCH_ROWS):
+                for h in range(2):
+                    n = WAVES * w + h
+                    w_codes, w_scales = code_tiles[ORDER[n]]
+                    nc.tensor.matmul_mx(
+                        out=p3_ps[:, a, :],
+                        lhsT=w_codes[:, a].rearrange("q h m -> q (h m)").bitcast(FP8X4),
+                        lhsT_scale=w_scales[:, a].rearrange("q h m -> q (h m)"),
+                        rhs=z_codes[:, n, :].bitcast(FP8X4),
+                        rhs_scale=z_scales[:, n, :],
+                        start=(h == 0),
+                        stop=(h == 1),
+                    )
+            state["p3", w] = p3_ps
+
+        def regroup(source_sb, name):
+            regrouped = keep.tile([P, K], BF16, name=name + "_regrouped")
+            nc.gpsimd.tensor_copy(
+                out=regrouped[:].bitcast(I32).rearrange("b (t h s j) -> b t h s j", t=SLOTS, h=2, s=STACK),
+                in_=source_sb[:].bitcast(I32).rearrange("b (s h t j) -> b t h s j", s=STACK, h=2, t=SLOTS),
+            )
+            return regrouped
+
+        def turn_slots(regrouped, turned):
+            for t in range(SLOTS):
+                nc.tensor.transpose(turned[:, t, :], regrouped[:, t * P : (t + 1) * P], identity_bf[:])
+
+        def times_x2(w):
+            slots = slice(PATCH_ROWS * w, PATCH_ROWS * (w + 1))
             nc.vector.scalar_tensor_tensor(
-                out=doubled[:],
-                in0=p3_ps[:].rearrange("b c s -> b s c"),
+                out=doubled[:, slots, :].rearrange("p a b -> p (a b)"),
+                in0=state["p3", w][:].rearrange("p a b -> p (a b)"),
                 scalar=2.0,
-                in1=x2_by_group[:, g],
+                in1=x2_t[:, slots, :].rearrange("p a b -> p (a b)"),
                 op0=MULT,
                 op1=MULT,
             )
-            nc.vector.tensor_tensor(out=x3_by_group[:, g], in0=doubled[:], in1=x1_by_group[:, g], op=SUBTRACT)
 
-        cwT_ps = psum_t.tile([P, HALVES, O], F32, tag="transposed")
-        transpose_pass(nc, cwT_ps, every_second_word(cw_sb[:]), identity[:])
+        def minus_x1():
+            nc.vector.tensor_tensor(
+                out=x3_by_slot,
+                in0=doubled[:].rearrange("p t b -> p b t"),
+                in1=x1_ps[:].rearrange("p t b -> p b t"),
+                op=SUBTRACT,
+            )
+
+        ctx.enter_context(tc.manual_schedule())
+        maskT_ps = psum_t.tile([P, HALVES, P], F32, tag="transposed")
+        transpose_pass(nc, maskT_ps, every_second_word(mask_sb[:]), identity[:])
+        nc.scalar.copy(
+            out=grouped_words(mask_t[:]), in_=maskT_ps[:, :, : GROUPS * IN_GROUP].rearrange("q u r -> q r u")
+        )
+        turn_weight(0)
+        nc.scalar.copy(out=z_split[:], in_=z_sb[:].bitcast(F32).rearrange("b (q u) -> b u q", u=HALVES))
+        multiply_by_mask(0)
+        turn_weight(1)
+        turn_z(0)
+        turn_z(1)
+        multiply_by_mask(1)
+        quantize_weight(0)
+        turn_weight(2)
+        quantize_z(0)
+        quantize_weight(1)
+        turn_z(2)
+        multiply_by_mask(2)
+        turn_weight(3)
+        turn_z(3)
+        quantize_weight(2)
+        multiply_by_mask(3)
+        quantize_z(1)
+        quantize_weight(3)
+        x2_regrouped = regroup(x2_sb, "x2")
+        x2_turned = psum_t.tile([P, SLOTS, B], BF16, tag="transposed")
+        turn_slots(x2_regrouped, x2_turned)
+        nc.scalar.copy(
+            out=x2_t[:].rearrange("p t b -> p (t b)").bitcast(F32), in_=x2_turned[:].rearrange("p t b -> p (t b)").bitcast(F32)
+        )
+        first_product(0)
+        x1_regrouped = regroup(x1_sb, "x1")
+        turn_slots(x1_regrouped, x1_ps)
+        cw_regrouped = regroup(cw_sb, "cw")
+        cw_turned = psum_t.tile([P, SLOTS, O], BF16, tag="transposed")
+        turn_slots(cw_regrouped, cw_turned)
         cw_grouped = keep.tile([P, O * PACK], BF16, align_bytes=64)
-        nc.scalar.copy(out=grouped_words(cw_grouped[:]), in_=cwT_ps[:].rearrange("q u r -> q r u"))
+        nc.scalar.copy(out=cw_grouped[:].rearrange("p (o t) -> p o t", t=SLOTS), in_=cw_turned[:].rearrange("p t o -> p o t"))
+        first_product(1)
+        times_x2(0)
         cw_codes = keep.tile([P, O], U32, align_bytes=64)
         cw_scales = keep.tile([P, O], U8, align_bytes=64)
         nc.vector.quantize_mx(out=cw_codes[:].bitcast(FP8X4), scales=cw_scales[:], in_=cw_grouped[:])
+        times_x2(1)
+        minus_x1()
 
-        x3T_ps = psum_t.tile([P, HALVES, B], F32, tag="transposed")
-        transpose_pass(nc, x3T_ps, every_second_word(x3_sb[:]), identity[:])
-        x3_grouped = keep.tile([P, B * PACK], BF16, align_bytes=64)
-        nc.vector.tensor_copy(out=grouped_words(x3_grouped[:]), in_=x3T_ps[:].rearrange("q u r -> q r u"))
         x3_codes = keep.tile([P, B], U32, align_bytes=64)
         x3_scales = keep.tile([P, B], U8, align_bytes=64)
         nc.vector.quantize_mx(out=x3_codes[:].bitcast(FP8X4), scales=x3_scales[:], in_=x3_grouped[:])
 
-        out_ps = psum.tile([B, O], F32)
+        out_ps = psum_x.tile([B, O], F32, tag="sums")
         nc.tensor.matmul_mx(
             out=out_ps[:],
             lhsT=x3_codes[:].bitcast(FP8X4),

@@ -59,7 +59,6 @@ HALF = P // 2
 SLOTS = PACK
 ORDER = (0, 2, 1, 3)
 WAVES = 2
-WARM_PASSES = 8
 
 
 def tile_chebyshev_l3_sparsed32_stack_pb_s_kernel(tc, z, T3, mask, x1, x2, C_w, C_b, out):
@@ -71,23 +70,6 @@ def tile_chebyshev_l3_sparsed32_stack_pb_s_kernel(tc, z, T3, mask, x1, x2, C_w, 
         psum = ctx.enter_context(tc.psum_pool(name="psum", bufs=1))
         psum_x = ctx.enter_context(tc.psum_pool(name="psum_x", bufs=2))
         psum_t = ctx.enter_context(tc.psum_pool(name="psum_t", bufs=4))
-
-        idle_grouped = keep.tile([P, P * PACK], BF16, align_bytes=64)
-        nc.vector.memset(idle_grouped[:].bitcast(F32), 0.0)
-        idle_codes = keep.tile([P, P], U32, align_bytes=64)
-        idle_scales = keep.tile([P, P], U8, align_bytes=64)
-        nc.vector.quantize_mx(out=idle_codes[:].bitcast(FP8X4), scales=idle_scales[:], in_=idle_grouped[:])
-        idle_ps = psum.tile([P, P], F32)
-        for n in range(WARM_PASSES):
-            nc.tensor.matmul_mx(
-                out=idle_ps[:],
-                lhsT=idle_codes[:].bitcast(FP8X4),
-                lhsT_scale=idle_scales[:],
-                rhs=idle_codes[:].bitcast(FP8X4),
-                rhs_scale=idle_scales[:],
-                start=True,
-                stop=True,
-            )
 
         identity = keep.tile([P, P], F32)
         make_identity(nc, identity[:])

@@ -235,16 +235,16 @@ def tile_chebyshev_l3_sparsed32_stack_pb_s_kernel(tc, z, T3, mask, x1, x2, C_w, 
         turn_z(1)
         multiply_by_mask(1)
         quantize_weight(0)
-        turn_weight(2)
+        turn_z(2)
         quantize_z(0)
         quantize_weight(1)
-        turn_z(2)
-        multiply_by_mask(2)
-        turn_weight(3)
         turn_z(3)
+        turn_weight(2)
+        multiply_by_mask(2)
+        quantize_z(1)
+        turn_weight(3)
         quantize_weight(2)
         multiply_by_mask(3)
-        quantize_z(1)
         quantize_weight(3)
         x2_regrouped = regroup(x2_sb, "x2")
         x2_turned = psum_t.tile([P, SLOTS, B], BF16, tag="transposed")

@@ -221,7 +221,6 @@ def tile_chebyshev_l3_sparsed32_stack_pb_s_kernel(tc, z, T3, mask, x1, x2, C_w, 
                 op=SUBTRACT,
             )
 
-        ctx.enter_context(tc.manual_schedule())
         maskT_ps = psum_t.tile([P, HALVES, P], F32, tag="transposed")
         transpose_pass(nc, maskT_ps, every_second_word(mask_sb[:]), identity[:])
         nc.scalar.copy(

@@ -68,7 +68,7 @@ def tile_chebyshev_l3_sparsed32_stack_pb_s_kernel(tc, z, T3, mask, x1, x2, C_w, 
         loads = ctx.enter_context(tc.tile_pool(name="loads", bufs=GROUPS))
         work = ctx.enter_context(tc.tile_pool(name="work", bufs=GROUPS))
         psum = ctx.enter_context(tc.psum_pool(name="psum", bufs=1))
-        psum_x = ctx.enter_context(tc.psum_pool(name="psum_x", bufs=2))
+        psum_x = ctx.enter_context(tc.psum_pool(name="psum_x", bufs=3))
         psum_t = ctx.enter_context(tc.psum_pool(name="psum_t", bufs=4))
 
         identity = keep.tile([P, P], F32)
@@ -173,22 +173,25 @@ def tile_chebyshev_l3_sparsed32_stack_pb_s_kernel(tc, z, T3, mask, x1, x2, C_w, 
                 in_=z_grouped[:, pair, :].rearrange("q n x -> q (n x)"),
             )
 
-        def first_product(w):
-            p3_ps = psum_x.tile([P, PATCH_ROWS, B], F32, tag="sums")
+        def open_slots():
+            shared = psum_x.tile([P, PATCH_ROWS, B], F32, tag="sums")
             for a in range(PATCH_ROWS):
-                for h in range(2):
-                    n = WAVES * w + h
-                    w_codes, w_scales = code_tiles[ORDER[n]]
-                    nc.tensor.matmul_mx(
-                        out=p3_ps[:, a, :],
-                        lhsT=w_codes[:, a].rearrange("q h m -> q (h m)").bitcast(FP8X4),
-                        lhsT_scale=w_scales[:, a].rearrange("q h m -> q (h m)"),
-                        rhs=z_codes[:, n, :].bitcast(FP8X4),
-                        rhs_scale=z_scales[:, n, :],
-                        start=(h == 0),
-                        stop=(h == 1),
-                    )
-            state["p3", w] = p3_ps
+                state["p3", 0, a] = shared[:, a, :]
+                own = psum_x.tile([P, B], F32, tag="sums", name="p3_own" + str(a))
+                state["p3", 1, a] = own[:]
+
+        def first_product(w, a, h):
+            n = WAVES * w + h
+            w_codes, w_scales = code_tiles[ORDER[n]]
+            nc.tensor.matmul_mx(
+                out=state["p3", w, a],
+                lhsT=w_codes[:, a].rearrange("q h m -> q (h m)").bitcast(FP8X4),
+                lhsT_scale=w_scales[:, a].rearrange("q h m -> q (h m)"),
+                rhs=z_codes[:, n, :].bitcast(FP8X4),
+                rhs_scale=z_scales[:, n, :],
+                start=(h == 0),
+                stop=(h == 1),
+            )
 
         def regroup(source_sb, name):
             regrouped = keep.tile([P, K], BF16, name=name + "_regrouped")
@@ -203,15 +206,11 @@ def tile_chebyshev_l3_sparsed32_stack_pb_s_kernel(tc, z, T3, mask, x1, x2, C_w, 
                 nc.tensor.transpose(turned[:, t, :], regrouped[:, t * P : (t + 1) * P], identity_bf[:])
 
         def times_x2(w):
-            slots = slice(PATCH_ROWS * w, PATCH_ROWS * (w + 1))
-            nc.vector.scalar_tensor_tensor(
-                out=doubled[:, slots, :].rearrange("p a b -> p (a b)"),
-                in0=state["p3", w][:].rearrange("p a b -> p (a b)"),
-                scalar=2.0,
-                in1=x2_t[:, slots, :].rearrange("p a b -> p (a b)"),
-                op0=MULT,
-                op1=MULT,
-            )
+            for a in range(PATCH_ROWS):
+                t = PATCH_ROWS * w + a
+                nc.vector.scalar_tensor_tensor(
+                    out=doubled[:, t, :], in0=state["p3", w, a], scalar=2.0, in1=x2_t[:, t, :], op0=MULT, op1=MULT
+                )
 
         def minus_x1():
             nc.vector.tensor_tensor(
@@ -221,6 +220,7 @@ def tile_chebyshev_l3_sparsed32_stack_pb_s_kernel(tc, z, T3, mask, x1, x2, C_w, 
                 op=SUBTRACT,
             )
 
+        open_slots()
         maskT_ps = psum_t.tile([P, HALVES, P], F32, tag="transposed")
         transpose_pass(nc, maskT_ps, every_second_word(mask_sb[:]), identity[:])
         nc.scalar.copy(
@@ -251,7 +251,11 @@ def tile_chebyshev_l3_sparsed32_stack_pb_s_kernel(tc, z, T3, mask, x1, x2, C_w, 
         nc.scalar.copy(
             out=x2_t[:].rearrange("p t b -> p (t b)").bitcast(F32), in_=x2_turned[:].rearrange("p t b -> p (t b)").bitcast(F32)
         )
-        first_product(0)
+        for a in range(PATCH_ROWS):
+            first_product(0, a, 0)
+            first_product(0, a, 1)
+        for a in range(PATCH_ROWS):
+            first_product(1, a, 0)
         x1_regrouped = regroup(x1_sb, "x1")
         turn_slots(x1_regrouped, x1_ps)
         cw_regrouped = regroup(cw_sb, "cw")
@@ -259,7 +263,8 @@ def tile_chebyshev_l3_sparsed32_stack_pb_s_kernel(tc, z, T3, mask, x1, x2, C_w, 
         turn_slots(cw_regrouped, cw_turned)
         cw_grouped = keep.tile([P, O * PACK], BF16, align_bytes=64)
         nc.scalar.copy(out=cw_grouped[:].rearrange("p (o t) -> p o t", t=SLOTS), in_=cw_turned[:].rearrange("p t o -> p o t"))
-        first_product(1)
+        for a in range(PATCH_ROWS):
+            first_product(1, a, 1)
         times_x2(0)
         cw_codes = keep.tile([P, O], U32, align_bytes=64)
         cw_scales = keep.tile([P, O], U8, align_bytes=64)

@@ -32,13 +32,17 @@ GROUPS = K // P
 PATCH_ROWS = POS // GROUPS
 IN_GROUP = PATCH_ROWS * POS
 WINDOW_ROWS = K_PASS // D
-assert STRIDE * (PATCH_ROWS - 1) + KW <= WINDOW_ROWS
+NEEDED = D * (STRIDE * (PATCH_ROWS - 1) + KW)
+assert NEEDED <= K_PASS
+WINDOW_STEP = D * PATCH_ROWS * STRIDE
+BEYOND = (GROUPS - 1) * WINDOW_STEP + K_PASS - D * D
+assert 0 <= BEYOND <= K_PASS - NEEDED
 
 FLOPS = 2 * B * D * D * K + 2 * B * K * O
 
 
 def window_start(g):
-    return D * min(g * PATCH_ROWS * STRIDE, D - WINDOW_ROWS)
+    return g * WINDOW_STEP
 
 
 def every_second_word(source):
@@ -82,19 +86,26 @@ def tile_chebyshev_l3_sparsed32_stack_pb_s_kernel(tc, z, T3, mask, x1, x2, C_w, 
         make_identity(nc, identity_bf[:])
 
         mask_sb = keep.tile([P, K_PASS], BF16)
-        nc.vector.memset(mask_sb[GROUPS * IN_GROUP :, :].bitcast(F32), 0.0)
-        for g in range(GROUPS):
-            window = slice(window_start(g), window_start(g) + K_PASS)
-            rows = slice(g * IN_GROUP, (g + 1) * IN_GROUP)
-            nc.sync.dma_start(out=mask_sb[rows, :], in_=mask[rows, window])
+        mask_rows = GROUPS * IN_GROUP
+        nc.vector.memset(mask_sb[mask_rows:, :].bitcast(F32), 0.0)
+        nc.vector.memset(mask_sb[:mask_rows, NEEDED:].bitcast(F32), 0.0)
+        group_step = IN_GROUP * D * D + WINDOW_STEP
+        mask_windows = (
+            mask.rearrange("r w -> (r w)")[: GROUPS * group_step]
+            .rearrange("(g y) -> g y", g=GROUPS)[:, : IN_GROUP * D * D]
+            .rearrange("g (c w) -> c g w", c=IN_GROUP)[:, :, :NEEDED]
+        )
+        nc.sync.dma_start(out=mask_sb[:mask_rows, :NEEDED], in_=mask_windows)
         t3_groups = T3.rearrange("(s g c) w -> g c s w", s=STACK, g=GROUPS)
         t3_tiles = {}
         z_sb = keep.tile([B, D * D], BF16)
 
         def load_group(g):
-            window = slice(window_start(g), window_start(g) + K_PASS)
+            inside = min(K_PASS, D * D - window_start(g))
             t3_sb = loads.tile([P, K_PASS], BF16)
-            nc.sync.dma_start(out=t3_sb[:], in_=t3_groups[g, :, :, window])
+            if inside < K_PASS:
+                nc.vector.memset(t3_sb[:, inside:].bitcast(F32), 0.0)
+            nc.sync.dma_start(out=t3_sb[:, :inside], in_=t3_groups[g, :, :, window_start(g) : window_start(g) + inside])
             t3_tiles[g] = t3_sb
 
         load_group(ORDER[0])
@@ -119,7 +130,8 @@ def tile_chebyshev_l3_sparsed32_stack_pb_s_kernel(tc, z, T3, mask, x1, x2, C_w, 
             nc.vector.memset(w_scales[:].rearrange("q a h m -> q (a h m)").bitcast(I32), 0)
             code_tiles[g] = (w_codes, w_scales)
 
-        z_split = keep.tile([B, HALVES, D * D // PACK], F32)
+        z_split = keep.tile([B, HALVES, (D * D + BEYOND) // PACK], F32)
+        nc.vector.memset(z_split[:, :, D * D // PACK :], 0.0)
         z_grouped = keep.tile([P, GROUPS, B * PACK], BF16, align_bytes=64)
         z_codes = keep.tile([P, GROUPS, B], U32, align_bytes=64)
         z_scales = keep.tile([P, GROUPS, B], U8, align_bytes=64)
@@ -224,10 +236,13 @@ def tile_chebyshev_l3_sparsed32_stack_pb_s_kernel(tc, z, T3, mask, x1, x2, C_w, 
         maskT_ps = psum_t.tile([P, HALVES, P], F32, tag="transposed")
         transpose_pass(nc, maskT_ps, every_second_word(mask_sb[:]), identity[:])
         nc.scalar.copy(
-            out=grouped_words(mask_t[:]), in_=maskT_ps[:, :, : GROUPS * IN_GROUP].rearrange("q u r -> q r u")
+            out=mask_t[:].bitcast(F32).rearrange("q (g c u) -> q g c u", g=GROUPS, u=HALVES),
+            in_=maskT_ps[:, :, :mask_rows].rearrange("q u (c g) -> q g c u", g=GROUPS),
         )
         turn_weight(0)
-        nc.scalar.copy(out=z_split[:], in_=z_sb[:].bitcast(F32).rearrange("b (q u) -> b u q", u=HALVES))
+        nc.scalar.copy(
+            out=z_split[:, :, : D * D // PACK], in_=z_sb[:].bitcast(F32).rearrange("b (q u) -> b u q", u=HALVES)
+        )
         multiply_by_mask(0)
         turn_weight(1)
         turn_z(0)

@@ -59,7 +59,9 @@ def grouped_words(grouped):
     return grouped.bitcast(F32).rearrange("q (r u) -> q r u", u=HALVES)
 
 
-HALF = P // 2
+UNITS = 2
+HALF = P // UNITS
+OCTET = IN_GROUP // UNITS
 SLOTS = PACK
 ORDER = (0, 2, 1, 3)
 WAVES = 2
@@ -78,12 +80,10 @@ def tile_chebyshev_l3_sparsed32_stack_pb_s_kernel(tc, z, T3, mask, x1, x2, C_w, 
         identity = keep.tile([P, P], F32)
         make_identity(nc, identity[:])
         swap = keep.tile([P, P], F32)
-        nc.gpsimd.tensor_copy(
-            out=swap[:].rearrange("r (a s j) -> r a s j", a=PATCH_ROWS, s=STACK),
-            in_=identity[:].rearrange("r (a j s) -> r a s j", a=PATCH_ROWS, s=STACK),
+        nc.vector.tensor_copy(
+            out=swap[:].rearrange("r (v s x) -> r v s x", v=UNITS, s=STACK),
+            in_=identity[:].rearrange("r (x v s) -> r v s x", v=UNITS, s=STACK),
         )
-        identity_bf = keep.tile([P, P], BF16)
-        make_identity(nc, identity_bf[:])
 
         mask_sb = keep.tile([P, K_PASS], BF16)
         mask_rows = GROUPS * IN_GROUP
@@ -124,8 +124,8 @@ def tile_chebyshev_l3_sparsed32_stack_pb_s_kernel(tc, z, T3, mask, x1, x2, C_w, 
 
         code_tiles = {}
         for g in ORDER:
-            w_codes = work.tile([P, PATCH_ROWS, 2, HALF], U32, align_bytes=64)
-            w_scales = work.tile([P, PATCH_ROWS, 2, HALF], U8, align_bytes=64)
+            w_codes = work.tile([P, UNITS, 2, HALF], U32, align_bytes=64)
+            w_scales = work.tile([P, UNITS, 2, HALF], U8, align_bytes=64)
             nc.vector.memset(w_codes[:, :, 1 - g // 2, :].bitcast(I32), 0)
             nc.vector.memset(w_scales[:].rearrange("q a h m -> q (a h m)").bitcast(I32), 0)
             code_tiles[g] = (w_codes, w_scales)
@@ -136,11 +136,10 @@ def tile_chebyshev_l3_sparsed32_stack_pb_s_kernel(tc, z, T3, mask, x1, x2, C_w, 
         z_codes = keep.tile([P, GROUPS, B], U32, align_bytes=64)
         z_scales = keep.tile([P, GROUPS, B], U8, align_bytes=64)
         mask_t = keep.tile([P, GROUPS * IN_GROUP * PACK], BF16)
-        mask_by_group = mask_t[:].rearrange("q (g a j u e) -> q g a j u e", g=GROUPS, a=PATCH_ROWS, u=HALVES, e=PAIR)
+        mask_by_group = mask_t[:].rearrange("q (g v x u e) -> q g v x u e", g=GROUPS, v=UNITS, u=HALVES, e=PAIR)
         x3_grouped = keep.tile([P, B * PACK], BF16, align_bytes=64)
-        x3_by_slot = x3_grouped[:].rearrange("p (b t) -> p b t", t=SLOTS)
-        x2_t = keep.tile([P, SLOTS, B], BF16)
-        x1_ps = psum.tile([P, SLOTS, B], BF16)
+        x2_t = keep.tile([P, WAVES, B, UNITS], BF16)
+        x1_ps = psum.tile([P, WAVES, B], F32)
         doubled = keep.tile([P, SLOTS, B], F32)
         state = {}
 
@@ -158,10 +157,10 @@ def tile_chebyshev_l3_sparsed32_stack_pb_s_kernel(tc, z, T3, mask, x1, x2, C_w, 
         def multiply_by_mask(n):
             g = ORDER[n]
             w_grouped = work.tile([P, P * PACK], BF16, align_bytes=64)
-            shape = [P, PATCH_ROWS, STACK, POS, HALVES, PAIR]
+            shape = [P, UNITS, STACK, OCTET, HALVES, PAIR]
             nc.vector.tensor_tensor(
-                out=w_grouped[:].rearrange("q (a s j u e) -> q a s j u e", a=PATCH_ROWS, s=STACK, u=HALVES, e=PAIR),
-                in0=state["wT", n][:].bitcast(BF16).rearrange("q u (a s j e) -> q a s j u e", a=PATCH_ROWS, s=STACK, e=PAIR),
+                out=w_grouped[:].rearrange("q (v s x u e) -> q v s x u e", v=UNITS, s=STACK, u=HALVES, e=PAIR),
+                in0=state["wT", n][:].bitcast(BF16).rearrange("q u (v s x e) -> q v s x u e", v=UNITS, s=STACK, e=PAIR),
                 in1=mask_by_group[:, g].unsqueeze(2).to_broadcast(shape),
                 op=MULT,
             )
@@ -170,11 +169,11 @@ def tile_chebyshev_l3_sparsed32_stack_pb_s_kernel(tc, z, T3, mask, x1, x2, C_w, 
         def quantize_weight(n):
             g = ORDER[n]
             w_codes, w_scales = code_tiles[g]
-            for a in range(PATCH_ROWS):
+            for v in range(UNITS):
                 nc.vector.quantize_mx(
-                    out=w_codes[:, a, g // 2, :].bitcast(FP8X4),
-                    scales=w_scales[:, a, g // 2, :],
-                    in_=state["w", n][:, a * HALF * PACK : (a + 1) * HALF * PACK],
+                    out=w_codes[:, v, g // 2, :].bitcast(FP8X4),
+                    scales=w_scales[:, v, g // 2, :],
+                    in_=state["w", n][:, v * HALF * PACK : (v + 1) * HALF * PACK],
                 )
 
         def quantize_z(w):
@@ -186,19 +185,19 @@ def tile_chebyshev_l3_sparsed32_stack_pb_s_kernel(tc, z, T3, mask, x1, x2, C_w, 
             )
 
         def open_slots():
-            shared = psum_x.tile([P, PATCH_ROWS, B], F32, tag="sums")
-            for a in range(PATCH_ROWS):
-                state["p3", 0, a] = shared[:, a, :]
-                own = psum_x.tile([P, B], F32, tag="sums", name="p3_own" + str(a))
-                state["p3", 1, a] = own[:]
+            shared = psum_x.tile([P, UNITS, B], F32, tag="sums")
+            for v in range(UNITS):
+                state["p3", 0, v] = shared[:, v, :]
+                own = psum_x.tile([P, B], F32, tag="sums", name="p3_own" + str(v))
+                state["p3", 1, v] = own[:]
 
-        def first_product(w, a, h):
+        def first_product(w, v, h):
             n = WAVES * w + h
             w_codes, w_scales = code_tiles[ORDER[n]]
             nc.tensor.matmul_mx(
-                out=state["p3", w, a],
-                lhsT=w_codes[:, a].rearrange("q h m -> q (h m)").bitcast(FP8X4),
-                lhsT_scale=w_scales[:, a].rearrange("q h m -> q (h m)"),
+                out=state["p3", w, v],
+                lhsT=w_codes[:, v].rearrange("q h m -> q (h m)").bitcast(FP8X4),
+                lhsT_scale=w_scales[:, v].rearrange("q h m -> q (h m)"),
                 rhs=z_codes[:, n, :].bitcast(FP8X4),
                 rhs_scale=z_scales[:, n, :],
                 start=(h == 0),
@@ -208,27 +207,32 @@ def tile_chebyshev_l3_sparsed32_stack_pb_s_kernel(tc, z, T3, mask, x1, x2, C_w, 
         def regroup(source_sb, name):
             regrouped = keep.tile([P, K], BF16, name=name + "_regrouped")
             nc.gpsimd.tensor_copy(
-                out=regrouped[:].bitcast(I32).rearrange("b (t h s j) -> b t h s j", t=SLOTS, h=2, s=STACK),
-                in_=source_sb[:].bitcast(I32).rearrange("b (s h t j) -> b t h s j", s=STACK, h=2, t=SLOTS),
+                out=regrouped[:].bitcast(I32).rearrange("b (w h s x) -> b w h s x", w=WAVES, h=2, s=STACK),
+                in_=source_sb[:].bitcast(I32).rearrange("b (s h w x) -> b w h s x", s=STACK, h=2, w=WAVES),
             )
             return regrouped
 
-        def turn_slots(regrouped, turned):
-            for t in range(SLOTS):
-                nc.tensor.transpose(turned[:, t, :], regrouped[:, t * P : (t + 1) * P], identity_bf[:])
+        def turn_words(regrouped, turned):
+            words = regrouped[:].bitcast(F32)
+            for w in range(WAVES):
+                nc.tensor.transpose(turned[:, w, :], words[:, w * P : (w + 1) * P], identity[:])
 
         def times_x2(w):
-            for a in range(PATCH_ROWS):
-                t = PATCH_ROWS * w + a
+            for v in range(UNITS):
                 nc.vector.scalar_tensor_tensor(
-                    out=doubled[:, t, :], in0=state["p3", w, a], scalar=2.0, in1=x2_t[:, t, :], op0=MULT, op1=MULT
+                    out=doubled[:, UNITS * w + v, :],
+                    in0=state["p3", w, v],
+                    scalar=2.0,
+                    in1=x2_t[:, w, :, v],
+                    op0=MULT,
+                    op1=MULT,
                 )
 
         def minus_x1():
             nc.vector.tensor_tensor(
-                out=x3_by_slot,
-                in0=doubled[:].rearrange("p t b -> p b t"),
-                in1=x1_ps[:].rearrange("p t b -> p b t"),
+                out=x3_grouped[:].rearrange("p (b w v) -> p b w v", w=WAVES, v=UNITS),
+                in0=doubled[:].rearrange("p (w v) b -> p b w v", v=UNITS),
+                in1=x1_ps[:].bitcast(BF16).rearrange("p w (b v) -> p b w v", v=UNITS),
                 op=SUBTRACT,
             )
 
@@ -236,8 +240,8 @@ def tile_chebyshev_l3_sparsed32_stack_pb_s_kernel(tc, z, T3, mask, x1, x2, C_w, 
         maskT_ps = psum_t.tile([P, HALVES, P], F32, tag="transposed")
         transpose_pass(nc, maskT_ps, every_second_word(mask_sb[:]), identity[:])
         nc.scalar.copy(
-            out=mask_t[:].bitcast(F32).rearrange("q (g c u) -> q g c u", g=GROUPS, u=HALVES),
-            in_=maskT_ps[:, :, :mask_rows].rearrange("q u (c g) -> q g c u", g=GROUPS),
+            out=mask_t[:].bitcast(F32).rearrange("q (g v x u) -> q g v x u", g=GROUPS, v=UNITS, u=HALVES),
+            in_=maskT_ps[:, :, :mask_rows].rearrange("q u (x v g) -> q g v x u", v=UNITS, g=GROUPS),
         )
         turn_weight(0)
         nc.scalar.copy(
@@ -261,25 +265,27 @@ def tile_chebyshev_l3_sparsed32_stack_pb_s_kernel(tc, z, T3, mask, x1, x2, C_w, 
         multiply_by_mask(3)
         quantize_weight(3)
         x2_regrouped = regroup(x2_sb, "x2")
-        x2_turned = psum_t.tile([P, SLOTS, B], BF16, tag="transposed")
-        turn_slots(x2_regrouped, x2_turned)
+        x2_turned = psum_t.tile([P, WAVES, B], F32, tag="transposed")
+        turn_words(x2_regrouped, x2_turned)
         nc.scalar.copy(
-            out=x2_t[:].rearrange("p t b -> p (t b)").bitcast(F32), in_=x2_turned[:].rearrange("p t b -> p (t b)").bitcast(F32)
+            out=x2_t[:].rearrange("p w b v -> p (w b v)").bitcast(F32), in_=x2_turned[:].rearrange("p w b -> p (w b)")
         )
-        for a in range(PATCH_ROWS):
-            first_product(0, a, 0)
-            first_product(0, a, 1)
-        for a in range(PATCH_ROWS):
-            first_product(1, a, 0)
+        for v in range(UNITS):
+            first_product(0, v, 0)
+            first_product(0, v, 1)
+        for v in range(UNITS):
+            first_product(1, v, 0)
         x1_regrouped = regroup(x1_sb, "x1")
-        turn_slots(x1_regrouped, x1_ps)
+        turn_words(x1_regrouped, x1_ps)
         cw_regrouped = regroup(cw_sb, "cw")
-        cw_turned = psum_t.tile([P, SLOTS, O], BF16, tag="transposed")
-        turn_slots(cw_regrouped, cw_turned)
+        cw_turned = psum_t.tile([P, WAVES, O], F32, tag="transposed")
+        turn_words(cw_regrouped, cw_turned)
         cw_grouped = keep.tile([P, O * PACK], BF16, align_bytes=64)
-        nc.scalar.copy(out=cw_grouped[:].rearrange("p (o t) -> p o t", t=SLOTS), in_=cw_turned[:].rearrange("p t o -> p o t"))
-        for a in range(PATCH_ROWS):
-            first_product(1, a, 1)
+        nc.scalar.copy(
+            out=cw_grouped[:].bitcast(F32).rearrange("p (o w) -> p o w", w=WAVES), in_=cw_turned[:].rearrange("p w o -> p o w")
+        )
+        for v in range(UNITS):
+            first_product(1, v, 1)
         times_x2(0)
         cw_codes = keep.tile([P, O], U32, align_bytes=64)
         cw_scales = keep.tile([P, O], U8, align_bytes=64)

@@ -109,8 +109,8 @@ def tile_chebyshev_l3_sparsed32_stack_pb_s_kernel(tc, z, T3, mask, x1, x2, C_w, 
             t3_tiles[g] = t3_sb
 
         load_group(ORDER[0])
-        nc.sync.dma_start(out=z_sb[:], in_=z)
         load_group(ORDER[1])
+        nc.sync.dma_start(out=z_sb[:], in_=z)
         load_group(ORDER[2])
         load_group(ORDER[3])
         x2_sb = keep.tile([B, K], BF16)
@@ -176,12 +176,12 @@ def tile_chebyshev_l3_sparsed32_stack_pb_s_kernel(tc, z, T3, mask, x1, x2, C_w, 
                     in_=state["w", n][:, v * HALF * PACK : (v + 1) * HALF * PACK],
                 )
 
-        def quantize_z(w):
-            pair = slice(WAVES * w, WAVES * (w + 1))
+        def quantize_z(first, count):
+            windows = slice(first, first + count)
             nc.vector.quantize_mx(
-                out=z_codes[:, pair, :].rearrange("q n b -> q (n b)").bitcast(FP8X4),
-                scales=z_scales[:, pair, :].rearrange("q n b -> q (n b)"),
-                in_=z_grouped[:, pair, :].rearrange("q n x -> q (n x)"),
+                out=z_codes[:, windows, :].rearrange("q n b -> q (n b)").bitcast(FP8X4),
+                scales=z_scales[:, windows, :].rearrange("q n b -> q (n b)"),
+                in_=z_grouped[:, windows, :].rearrange("q n x -> q (n x)"),
             )
 
         def open_slots():
@@ -239,7 +239,7 @@ def tile_chebyshev_l3_sparsed32_stack_pb_s_kernel(tc, z, T3, mask, x1, x2, C_w, 
         open_slots()
         maskT_ps = psum_t.tile([P, HALVES, P], F32, tag="transposed")
         transpose_pass(nc, maskT_ps, every_second_word(mask_sb[:]), identity[:])
-        nc.scalar.copy(
+        nc.vector.tensor_copy(
             out=mask_t[:].bitcast(F32).rearrange("q (g v x u) -> q g v x u", g=GROUPS, v=UNITS, u=HALVES),
             in_=maskT_ps[:, :, :mask_rows].rearrange("q u (x v g) -> q g v x u", v=UNITS, g=GROUPS),
         )
@@ -247,23 +247,24 @@ def tile_chebyshev_l3_sparsed32_stack_pb_s_kernel(tc, z, T3, mask, x1, x2, C_w, 
         nc.scalar.copy(
             out=z_split[:, :, : D * D // PACK], in_=z_sb[:].bitcast(F32).rearrange("b (q u) -> b u q", u=HALVES)
         )
-        multiply_by_mask(0)
         turn_weight(1)
-        turn_z(0)
-        turn_z(1)
+        multiply_by_mask(0)
+        turn_weight(2)
         multiply_by_mask(1)
         quantize_weight(0)
-        turn_z(2)
-        quantize_z(0)
-        quantize_weight(1)
-        turn_z(3)
-        turn_weight(2)
-        multiply_by_mask(2)
-        quantize_z(1)
         turn_weight(3)
-        quantize_weight(2)
+        multiply_by_mask(2)
+        quantize_weight(1)
+        turn_z(0)
         multiply_by_mask(3)
+        quantize_weight(2)
+        turn_z(1)
         quantize_weight(3)
+        turn_z(2)
+        quantize_z(0, 2)
+        turn_z(3)
+        quantize_z(2, 1)
+        quantize_z(3, 1)
         x2_regrouped = regroup(x2_sb, "x2")
         x2_turned = psum_t.tile([P, WAVES, B], F32, tag="transposed")
         turn_words(x2_regrouped, x2_turned)

@@ -271,13 +271,15 @@ def tile_chebyshev_l3_sparsed32_stack_pb_s_kernel(tc, z, T3, mask, x1, x2, C_w, 
         nc.scalar.copy(
             out=x2_t[:].rearrange("p w b v -> p (w b v)").bitcast(F32), in_=x2_turned[:].rearrange("p w b -> p (w b)")
         )
+        x1_regrouped = regroup(x1_sb, "x1")
+        turn_words(x1_regrouped, x1_ps)
         for v in range(UNITS):
             first_product(0, v, 0)
             first_product(0, v, 1)
         for v in range(UNITS):
             first_product(1, v, 0)
-        x1_regrouped = regroup(x1_sb, "x1")
-        turn_words(x1_regrouped, x1_ps)
+        for v in range(UNITS):
+            first_product(1, v, 1)
         cw_regrouped = regroup(cw_sb, "cw")
         cw_turned = psum_t.tile([P, WAVES, O], F32, tag="transposed")
         turn_words(cw_regrouped, cw_turned)
@@ -285,14 +287,12 @@ def tile_chebyshev_l3_sparsed32_stack_pb_s_kernel(tc, z, T3, mask, x1, x2, C_w, 
         nc.scalar.copy(
             out=cw_grouped[:].bitcast(F32).rearrange("p (o w) -> p o w", w=WAVES), in_=cw_turned[:].rearrange("p w o -> p o w")
         )
-        for v in range(UNITS):
-            first_product(1, v, 1)
         times_x2(0)
+        times_x2(1)
+        minus_x1()
         cw_codes = keep.tile([P, O], U32, align_bytes=64)
         cw_scales = keep.tile([P, O], U8, align_bytes=64)
         nc.vector.quantize_mx(out=cw_codes[:].bitcast(FP8X4), scales=cw_scales[:], in_=cw_grouped[:])
-        times_x2(1)
-        minus_x1()
 
         x3_codes = keep.tile([P, B], U32, align_bytes=64)
         x3_scales = keep.tile([P, B], U8, align_bytes=64)

@@ -110,13 +110,14 @@ def tile_chebyshev_l3_sparsed32_stack_pb_s_kernel(tc, z, T3, mask, x1, x2, C_w, 
 
         load_group(ORDER[0])
         load_group(ORDER[1])
-        nc.sync.dma_start(out=z_sb[:], in_=z)
+        nc.sync.dma_start(out=z_sb[:, :K_PASS], in_=z[:, :K_PASS])
         load_group(ORDER[2])
+        nc.sync.dma_start(out=z_sb[:, K_PASS:], in_=z[:, K_PASS:])
         load_group(ORDER[3])
-        x2_sb = keep.tile([B, K], BF16)
-        nc.sync.dma_start(out=x2_sb[:], in_=x2)
         x1_sb = keep.tile([B, K], BF16)
         nc.sync.dma_start(out=x1_sb[:], in_=x1)
+        x2_sb = keep.tile([B, K], BF16)
+        nc.sync.dma_start(out=x2_sb[:], in_=x2)
         cw_sb = keep.tile([O, K], BF16)
         nc.sync.dma_start(out=cw_sb[:], in_=C_w)
         bias_sb = keep.tile([B, O], BF16)
@@ -147,6 +148,12 @@ def tile_chebyshev_l3_sparsed32_stack_pb_s_kernel(tc, z, T3, mask, x1, x2, C_w, 
             wT_ps = psum_t.tile([P, HALVES, P], F32, tag="transposed")
             transpose_pass(nc, wT_ps, every_second_word(t3_tiles[ORDER[n]][:]), swap[:])
             state["wT", n] = wT_ps
+
+        def split_z(f):
+            nc.scalar.copy(
+                out=z_split[:, :, f * P : (f + 1) * P],
+                in_=z_sb[:, f * K_PASS : (f + 1) * K_PASS].bitcast(F32).rearrange("b (q u) -> b u q", u=HALVES),
+            )
 
         def turn_z(n):
             zT_ps = psum_t.tile([P, HALVES, B], F32, tag="transposed")
@@ -204,9 +211,9 @@ def tile_chebyshev_l3_sparsed32_stack_pb_s_kernel(tc, z, T3, mask, x1, x2, C_w, 
                 stop=(h == 1),
             )
 
-        def regroup(source_sb, name):
+        def regroup(engine, source_sb, name):
             regrouped = keep.tile([P, K], BF16, name=name + "_regrouped")
-            nc.gpsimd.tensor_copy(
+            engine.tensor_copy(
                 out=regrouped[:].bitcast(I32).rearrange("b (w h s x) -> b w h s x", w=WAVES, h=2, s=STACK),
                 in_=source_sb[:].bitcast(I32).rearrange("b (s h w x) -> b w h s x", s=STACK, h=2, w=WAVES),
             )
@@ -236,6 +243,7 @@ def tile_chebyshev_l3_sparsed32_stack_pb_s_kernel(tc, z, T3, mask, x1, x2, C_w, 
                 op=SUBTRACT,
             )
 
+        ctx.enter_context(tc.manual_schedule(engines={mybir.EngineType.DVE}))
         open_slots()
         maskT_ps = psum_t.tile([P, HALVES, P], F32, tag="transposed")
         transpose_pass(nc, maskT_ps, every_second_word(mask_sb[:]), identity[:])
@@ -244,34 +252,33 @@ def tile_chebyshev_l3_sparsed32_stack_pb_s_kernel(tc, z, T3, mask, x1, x2, C_w, 
             in_=maskT_ps[:, :, :mask_rows].rearrange("q u (x v g) -> q g v x u", v=UNITS, g=GROUPS),
         )
         turn_weight(0)
-        nc.scalar.copy(
-            out=z_split[:, :, : D * D // PACK], in_=z_sb[:].bitcast(F32).rearrange("b (q u) -> b u q", u=HALVES)
-        )
+        split_z(0)
         turn_weight(1)
         multiply_by_mask(0)
         turn_weight(2)
+        split_z(1)
         multiply_by_mask(1)
         quantize_weight(0)
+        turn_z(0)
         turn_weight(3)
         multiply_by_mask(2)
         quantize_weight(1)
-        turn_z(0)
+        turn_z(1)
         multiply_by_mask(3)
         quantize_weight(2)
-        turn_z(1)
-        quantize_weight(3)
+        x1_regrouped = regroup(nc.vector, x1_sb, "x1")
         turn_z(2)
+        quantize_weight(3)
         quantize_z(0, 2)
         turn_z(3)
         quantize_z(2, 1)
         quantize_z(3, 1)
-        x2_regrouped = regroup(x2_sb, "x2")
+        x2_regrouped = regroup(nc.gpsimd, x2_sb, "x2")
         x2_turned = psum_t.tile([P, WAVES, B], F32, tag="transposed")
         turn_words(x2_regrouped, x2_turned)
         nc.scalar.copy(
             out=x2_t[:].rearrange("p w b v -> p (w b v)").bitcast(F32), in_=x2_turned[:].rearrange("p w b -> p (w b)")
         )
-        x1_regrouped = regroup(x1_sb, "x1")
         turn_words(x1_regrouped, x1_ps)
         for v in range(UNITS):
             first_product(0, v, 0)
@@ -280,7 +287,7 @@ def tile_chebyshev_l3_sparsed32_stack_pb_s_kernel(tc, z, T3, mask, x1, x2, C_w, 
             first_product(1, v, 0)
         for v in range(UNITS):
             first_product(1, v, 1)
-        cw_regrouped = regroup(cw_sb, "cw")
+        cw_regrouped = regroup(nc.gpsimd, cw_sb, "cw")
         cw_turned = psum_t.tile([P, WAVES, O], F32, tag="transposed")
         turn_words(cw_regrouped, cw_turned)
         cw_grouped = keep.tile([P, O * PACK], BF16, align_bytes=64)

@@ -123,13 +123,14 @@ def tile_chebyshev_l3_sparsed32_stack_pb_s_kernel(tc, z, T3, mask, x1, x2, C_w, 
         bias_sb = keep.tile([B, O], BF16)
         nc.sync.dma_start(out=bias_sb[:], in_=C_b.partition_broadcast(B))
 
-        code_tiles = {}
-        for g in ORDER:
-            w_codes = work.tile([P, UNITS, 2, HALF], U32, align_bytes=64)
-            w_scales = work.tile([P, UNITS, 2, HALF], U8, align_bytes=64)
-            nc.vector.memset(w_codes[:, :, 1 - g // 2, :].bitcast(I32), 0)
-            nc.vector.memset(w_scales[:].rearrange("q a h m -> q (a h m)").bitcast(I32), 0)
-            code_tiles[g] = (w_codes, w_scales)
+        code_tiles = []
+        for w in range(WAVES):
+            w_codes = work.tile([P, UNITS, 4, HALF], U32, align_bytes=64)
+            w_scales = work.tile([P, UNITS, 4, HALF], U8, align_bytes=64)
+            nc.vector.memset(w_codes[:, :, 0, :].bitcast(I32), 0)
+            nc.vector.memset(w_codes[:, :, 3, :].bitcast(I32), 0)
+            nc.vector.memset(w_scales[:].rearrange("q v k m -> q (v k m)").bitcast(I32), 0)
+            code_tiles.append((w_codes, w_scales))
 
         z_split = keep.tile([B, HALVES, (D * D + BEYOND) // PACK], F32)
         nc.vector.memset(z_split[:, :, D * D // PACK :], 0.0)
@@ -162,25 +163,25 @@ def tile_chebyshev_l3_sparsed32_stack_pb_s_kernel(tc, z, T3, mask, x1, x2, C_w, 
             nc.scalar.copy(out=grouped_words(z_grouped[:, n, :]), in_=zT_ps[:].rearrange("q u r -> q r u"))
 
         def multiply_by_mask(n):
-            g = ORDER[n]
-            w_grouped = work.tile([P, P * PACK], BF16, align_bytes=64)
+            w, h = n // WAVES, n % WAVES
+            if h == 0:
+                w_grouped = work.tile([P, UNITS, WAVES, HALF * PACK], BF16, align_bytes=64)
+                state["w", w] = w_grouped
             shape = [P, UNITS, STACK, OCTET, HALVES, PAIR]
             nc.vector.tensor_tensor(
-                out=w_grouped[:].rearrange("q (v s x u e) -> q v s x u e", v=UNITS, s=STACK, u=HALVES, e=PAIR),
+                out=state["w", w][:, :, 1 - h, :].rearrange("q v (s x u e) -> q v s x u e", s=STACK, u=HALVES, e=PAIR),
                 in0=state["wT", n][:].bitcast(BF16).rearrange("q u (v s x e) -> q v s x u e", v=UNITS, s=STACK, e=PAIR),
-                in1=mask_by_group[:, g].unsqueeze(2).to_broadcast(shape),
+                in1=mask_by_group[:, ORDER[n]].unsqueeze(2).to_broadcast(shape),
                 op=MULT,
             )
-            state["w", n] = w_grouped
 
-        def quantize_weight(n):
-            g = ORDER[n]
-            w_codes, w_scales = code_tiles[g]
+        def quantize_weight(w):
+            w_codes, w_scales = code_tiles[w]
             for v in range(UNITS):
                 nc.vector.quantize_mx(
-                    out=w_codes[:, v, g // 2, :].bitcast(FP8X4),
-                    scales=w_scales[:, v, g // 2, :],
-                    in_=state["w", n][:, v * HALF * PACK : (v + 1) * HALF * PACK],
+                    out=w_codes[:, v, 1:3, :].rearrange("q k m -> q (k m)").bitcast(FP8X4),
+                    scales=w_scales[:, v, 1:3, :].rearrange("q k m -> q (k m)"),
+                    in_=state["w", w][:, v].rearrange("q k c -> q (k c)"),
                 )
 
         def quantize_z(first, count):
@@ -200,11 +201,12 @@ def tile_chebyshev_l3_sparsed32_stack_pb_s_kernel(tc, z, T3, mask, x1, x2, C_w, 
 
         def first_product(w, v, h):
             n = WAVES * w + h
-            w_codes, w_scales = code_tiles[ORDER[n]]
+            w_codes, w_scales = code_tiles[w]
+            blocks = slice(2 * (1 - h), 2 * (1 - h) + 2)
             nc.tensor.matmul_mx(
                 out=state["p3", w, v],
-                lhsT=w_codes[:, v].rearrange("q h m -> q (h m)").bitcast(FP8X4),
-                lhsT_scale=w_scales[:, v].rearrange("q h m -> q (h m)"),
+                lhsT=w_codes[:, v, blocks, :].rearrange("q k m -> q (k m)").bitcast(FP8X4),
+                lhsT_scale=w_scales[:, v, blocks, :].rearrange("q k m -> q (k m)"),
                 rhs=z_codes[:, n, :].bitcast(FP8X4),
                 rhs_scale=z_scales[:, n, :],
                 start=(h == 0),
@@ -258,17 +260,15 @@ def tile_chebyshev_l3_sparsed32_stack_pb_s_kernel(tc, z, T3, mask, x1, x2, C_w, 
         turn_weight(2)
         split_z(1)
         multiply_by_mask(1)
-        quantize_weight(0)
         turn_z(0)
         turn_weight(3)
         multiply_by_mask(2)
-        quantize_weight(1)
+        quantize_weight(0)
         turn_z(1)
         multiply_by_mask(3)
-        quantize_weight(2)
         x1_regrouped = regroup(nc.vector, x1_sb, "x1")
         turn_z(2)
-        quantize_weight(3)
+        quantize_weight(1)
         quantize_z(0, 2)
         turn_z(3)
         quantize_z(2, 1)

from contextlib import ExitStack

import concourse.mybir as mybir
from concourse.masks import make_identity

F32 = mybir.dt.float32
BF16 = mybir.dt.bfloat16
U32 = mybir.dt.uint32
U8 = mybir.dt.uint8
I32 = mybir.dt.int32
FP8X4 = mybir.dt.float8_e4m3fn_x4
MULT = mybir.AluOpType.mult
SUBTRACT = mybir.AluOpType.subtract
ADD = mybir.AluOpType.add

P = 128
PACK = 4
K_PASS = P * PACK
PAIR = 2
HALVES = PACK // PAIR

D = 32
KW = 11
STRIDE = 3
POS = 8
STACK = 8
B = 128
K = STACK * POS * POS
O = 128

GROUPS = K // P
PATCH_ROWS = POS // GROUPS
IN_GROUP = PATCH_ROWS * POS
WINDOW_ROWS = K_PASS // D
NEEDED = D * (STRIDE * (PATCH_ROWS - 1) + KW)
assert NEEDED <= K_PASS
WINDOW_STEP = D * PATCH_ROWS * STRIDE
BEYOND = (GROUPS - 1) * WINDOW_STEP + K_PASS - D * D
assert 0 <= BEYOND <= K_PASS - NEEDED

FLOPS = 2 * B * D * D * K + 2 * B * K * O


def window_start(g):
    return g * WINDOW_STEP


def every_second_word(source):
    words = source.bitcast(F32)
    return [words[:, u : K_PASS // PAIR : HALVES] for u in range(HALVES)]


def transpose_pass(nc, psum_view, word_blocks, identity):
    for u in range(HALVES):
        nc.tensor.transpose(psum_view[:, u, :], word_blocks[u], identity)


def grouped_words(grouped):
    return grouped.bitcast(F32).rearrange("q (r u) -> q r u", u=HALVES)


UNITS = 2
HALF = P // UNITS
OCTET = IN_GROUP // UNITS
SLOTS = PACK
ORDER = (0, 2, 1, 3)
WAVES = 2


def tile_chebyshev_l3_sparsed32_stack_pb_s_kernel(tc, z, T3, mask, x1, x2, C_w, C_b, out):
    nc = tc.nc
    with ExitStack() as ctx:
        keep = ctx.enter_context(tc.tile_pool(name="keep", bufs=1))
        loads = ctx.enter_context(tc.tile_pool(name="loads", bufs=GROUPS))
        work = ctx.enter_context(tc.tile_pool(name="work", bufs=GROUPS))
        psum = ctx.enter_context(tc.psum_pool(name="psum", bufs=1))
        psum_x = ctx.enter_context(tc.psum_pool(name="psum_x", bufs=3))
        psum_t = ctx.enter_context(tc.psum_pool(name="psum_t", bufs=4))

        identity = keep.tile([P, P], F32)
        make_identity(nc, identity[:])
        swap = keep.tile([P, P], F32)
        nc.vector.tensor_copy(
            out=swap[:].rearrange("r (v s x) -> r v s x", v=UNITS, s=STACK),
            in_=identity[:].rearrange("r (x v s) -> r v s x", v=UNITS, s=STACK),
        )

        mask_sb = keep.tile([P, K_PASS], BF16)
        mask_rows = GROUPS * IN_GROUP
        nc.vector.memset(mask_sb[mask_rows:, :].bitcast(F32), 0.0)
        nc.vector.memset(mask_sb[:mask_rows, NEEDED:].bitcast(F32), 0.0)
        group_step = IN_GROUP * D * D + WINDOW_STEP
        mask_windows = (
            mask.rearrange("r w -> (r w)")[: GROUPS * group_step]
            .rearrange("(g y) -> g y", g=GROUPS)[:, : IN_GROUP * D * D]
            .rearrange("g (c w) -> c g w", c=IN_GROUP)[:, :, :NEEDED]
        )
        nc.sync.dma_start(out=mask_sb[:mask_rows, :NEEDED], in_=mask_windows)
        t3_groups = T3.rearrange("(s g c) w -> g c s w", s=STACK, g=GROUPS)
        t3_tiles = {}
        z_sb = keep.tile([B, D * D], BF16)

        def load_group(g):
            inside = min(K_PASS, D * D - window_start(g))
            t3_sb = loads.tile([P, K_PASS], BF16)
            if inside < K_PASS:
                nc.vector.memset(t3_sb[:, inside:].bitcast(F32), 0.0)
            nc.sync.dma_start(out=t3_sb[:, :inside], in_=t3_groups[g, :, :, window_start(g) : window_start(g) + inside])
            t3_tiles[g] = t3_sb

        load_group(ORDER[0])
        load_group(ORDER[1])
        nc.sync.dma_start(out=z_sb[:, :K_PASS], in_=z[:, :K_PASS])
        load_group(ORDER[2])
        nc.sync.dma_start(out=z_sb[:, K_PASS:], in_=z[:, K_PASS:])
        load_group(ORDER[3])
        x1_sb = keep.tile([B, K], BF16)
        nc.sync.dma_start(out=x1_sb[:], in_=x1)
        x2_sb = keep.tile([B, K], BF16)
        nc.sync.dma_start(out=x2_sb[:], in_=x2)
        cw_sb = keep.tile([O, K], BF16)
        nc.sync.dma_start(out=cw_sb[:], in_=C_w)
        bias_sb = keep.tile([B, O], BF16)
        nc.sync.dma_start(out=bias_sb[:], in_=C_b.partition_broadcast(B))

        code_tiles = []
        for w in range(WAVES):
            w_codes = work.tile([P, UNITS, 4, HALF], U32, align_bytes=64)
            w_scales = work.tile([P, UNITS, 4, HALF], U8, align_bytes=64)
            nc.vector.memset(w_codes[:, :, 0, :].bitcast(I32), 0)
            nc.vector.memset(w_codes[:, :, 3, :].bitcast(I32), 0)
            nc.vector.memset(w_scales[:].rearrange("q v k m -> q (v k m)").bitcast(I32), 0)
            code_tiles.append((w_codes, w_scales))

        z_split = keep.tile([B, HALVES, (D * D + BEYOND) // PACK], F32)
        nc.vector.memset(z_split[:, :, D * D // PACK :], 0.0)
        z_grouped = keep.tile([P, GROUPS, B * PACK], BF16, align_bytes=64)
        z_codes = keep.tile([P, GROUPS, B], U32, align_bytes=64)
        z_scales = keep.tile([P, GROUPS, B], U8, align_bytes=64)
        mask_t = keep.tile([P, GROUPS * IN_GROUP * PACK], BF16)
        mask_by_group = mask_t[:].rearrange("q (g v x u e) -> q g v x u e", g=GROUPS, v=UNITS, u=HALVES, e=PAIR)
        x3_grouped = keep.tile([P, B * PACK], BF16, align_bytes=64)
        x2_t = keep.tile([P, WAVES, B, UNITS], BF16)
        x1_ps = psum.tile([P, WAVES, B], F32)
        doubled = keep.tile([P, SLOTS, B], F32)
        state = {}

        def turn_weight(n):
            wT_ps = psum_t.tile([P, HALVES, P], F32, tag="transposed")
            transpose_pass(nc, wT_ps, every_second_word(t3_tiles[ORDER[n]][:]), swap[:])
            state["wT", n] = wT_ps

        def split_z(f):
            nc.scalar.copy(
                out=z_split[:, :, f * P : (f + 1) * P],
                in_=z_sb[:, f * K_PASS : (f + 1) * K_PASS].bitcast(F32).rearrange("b (q u) -> b u q", u=HALVES),
            )

        def turn_z(n):
            zT_ps = psum_t.tile([P, HALVES, B], F32, tag="transposed")
            first = window_start(ORDER[n]) // PACK
            transpose_pass(nc, zT_ps, [z_split[:, u, first : first + P] for u in range(HALVES)], identity[:])
            nc.scalar.copy(out=grouped_words(z_grouped[:, n, :]), in_=zT_ps[:].rearrange("q u r -> q r u"))

        def multiply_by_mask(n):
            w, h = n // WAVES, n % WAVES
            if h == 0:
                w_grouped = work.tile([P, UNITS, WAVES, HALF * PACK], BF16, align_bytes=64)
                state["w", w] = w_grouped
            shape = [P, UNITS, STACK, OCTET, HALVES, PAIR]
            nc.vector.tensor_tensor(
                out=state["w", w][:, :, 1 - h, :].rearrange("q v (s x u e) -> q v s x u e", s=STACK, u=HALVES, e=PAIR),
                in0=state["wT", n][:].bitcast(BF16).rearrange("q u (v s x e) -> q v s x u e", v=UNITS, s=STACK, e=PAIR),
                in1=mask_by_group[:, ORDER[n]].unsqueeze(2).to_broadcast(shape),
                op=MULT,
            )

        def quantize_weight(w):
            w_codes, w_scales = code_tiles[w]
            for v in range(UNITS):
                nc.vector.quantize_mx(
                    out=w_codes[:, v, 1:3, :].rearrange("q k m -> q (k m)").bitcast(FP8X4),
                    scales=w_scales[:, v, 1:3, :].rearrange("q k m -> q (k m)"),
                    in_=state["w", w][:, v].rearrange("q k c -> q (k c)"),
                )

        def quantize_z(first, count):
            windows = slice(first, first + count)
            nc.vector.quantize_mx(
                out=z_codes[:, windows, :].rearrange("q n b -> q (n b)").bitcast(FP8X4),
                scales=z_scales[:, windows, :].rearrange("q n b -> q (n b)"),
                in_=z_grouped[:, windows, :].rearrange("q n x -> q (n x)"),
            )

        def open_slots():
            shared = psum_x.tile([P, UNITS, B], F32, tag="sums")
            for v in range(UNITS):
                state["p3", 0, v] = shared[:, v, :]
                own = psum_x.tile([P, B], F32, tag="sums", name="p3_own" + str(v))
                state["p3", 1, v] = own[:]

        def first_product(w, v, h):
            n = WAVES * w + h
            w_codes, w_scales = code_tiles[w]
            blocks = slice(2 * (1 - h), 2 * (1 - h) + 2)
            nc.tensor.matmul_mx(
                out=state["p3", w, v],
                lhsT=w_codes[:, v, blocks, :].rearrange("q k m -> q (k m)").bitcast(FP8X4),
                lhsT_scale=w_scales[:, v, blocks, :].rearrange("q k m -> q (k m)"),
                rhs=z_codes[:, n, :].bitcast(FP8X4),
                rhs_scale=z_scales[:, n, :],
                start=(h == 0),
                stop=(h == 1),
            )

        def regroup(engine, source_sb, name):
            regrouped = keep.tile([P, K], BF16, name=name + "_regrouped")
            engine.tensor_copy(
                out=regrouped[:].bitcast(I32).rearrange("b (w h s x) -> b w h s x", w=WAVES, h=2, s=STACK),
                in_=source_sb[:].bitcast(I32).rearrange("b (s h w x) -> b w h s x", s=STACK, h=2, w=WAVES),
            )
            return regrouped

        def turn_words(regrouped, turned):
            words = regrouped[:].bitcast(F32)
            for w in range(WAVES):
                nc.tensor.transpose(turned[:, w, :], words[:, w * P : (w + 1) * P], identity[:])

        def times_x2(w):
            for v in range(UNITS):
                nc.vector.scalar_tensor_tensor(
                    out=doubled[:, UNITS * w + v, :],
                    in0=state["p3", w, v],
                    scalar=2.0,
                    in1=x2_t[:, w, :, v],
                    op0=MULT,
                    op1=MULT,
                )

        def minus_x1():
            nc.vector.tensor_tensor(
                out=x3_grouped[:].rearrange("p (b w v) -> p b w v", w=WAVES, v=UNITS),
                in0=doubled[:].rearrange("p (w v) b -> p b w v", v=UNITS),
                in1=x1_ps[:].bitcast(BF16).rearrange("p w (b v) -> p b w v", v=UNITS),
                op=SUBTRACT,
            )

        ctx.enter_context(tc.manual_schedule(engines={mybir.EngineType.DVE}))
        open_slots()
        maskT_ps = psum_t.tile([P, HALVES, P], F32, tag="transposed")
        transpose_pass(nc, maskT_ps, every_second_word(mask_sb[:]), identity[:])
        nc.vector.tensor_copy(
            out=mask_t[:].bitcast(F32).rearrange("q (g v x u) -> q g v x u", g=GROUPS, v=UNITS, u=HALVES),
            in_=maskT_ps[:, :, :mask_rows].rearrange("q u (x v g) -> q g v x u", v=UNITS, g=GROUPS),
        )
        turn_weight(0)
        split_z(0)
        turn_weight(1)
        multiply_by_mask(0)
        turn_weight(2)
        split_z(1)
        multiply_by_mask(1)
        turn_z(0)
        turn_weight(3)
        multiply_by_mask(2)
        quantize_weight(0)
        turn_z(1)
        multiply_by_mask(3)
        x1_regrouped = regroup(nc.vector, x1_sb, "x1")
        turn_z(2)
        quantize_weight(1)
        quantize_z(0, 2)
        turn_z(3)
        quantize_z(2, 1)
        quantize_z(3, 1)
        x2_regrouped = regroup(nc.gpsimd, x2_sb, "x2")
        x2_turned = psum_t.tile([P, WAVES, B], F32, tag="transposed")
        turn_words(x2_regrouped, x2_turned)
        nc.scalar.copy(
            out=x2_t[:].rearrange("p w b v -> p (w b v)").bitcast(F32), in_=x2_turned[:].rearrange("p w b -> p (w b)")
        )
        turn_words(x1_regrouped, x1_ps)
        for v in range(UNITS):
            first_product(0, v, 0)
            first_product(0, v, 1)
        for v in range(UNITS):
            first_product(1, v, 0)
        for v in range(UNITS):
            first_product(1, v, 1)
        cw_regrouped = regroup(nc.gpsimd, cw_sb, "cw")
        cw_turned = psum_t.tile([P, WAVES, O], F32, tag="transposed")
        turn_words(cw_regrouped, cw_turned)
        cw_grouped = keep.tile([P, O * PACK], BF16, align_bytes=64)
        nc.scalar.copy(
            out=cw_grouped[:].bitcast(F32).rearrange("p (o w) -> p o w", w=WAVES), in_=cw_turned[:].rearrange("p w o -> p o w")
        )
        times_x2(0)
        times_x2(1)
        minus_x1()
        cw_codes = keep.tile([P, O], U32, align_bytes=64)
        cw_scales = keep.tile([P, O], U8, align_bytes=64)
        nc.vector.quantize_mx(out=cw_codes[:].bitcast(FP8X4), scales=cw_scales[:], in_=cw_grouped[:])

        x3_codes = keep.tile([P, B], U32, align_bytes=64)
        x3_scales = keep.tile([P, B], U8, align_bytes=64)
        nc.vector.quantize_mx(out=x3_codes[:].bitcast(FP8X4), scales=x3_scales[:], in_=x3_grouped[:])

        out_ps = psum_x.tile([B, O], F32, tag="sums")
        nc.tensor.matmul_mx(
            out=out_ps[:],
            lhsT=x3_codes[:].bitcast(FP8X4),
            lhsT_scale=x3_scales[:],
            rhs=cw_codes[:].bitcast(FP8X4),
            rhs_scale=cw_scales[:],
            start=True,
            stop=True,
        )
        out_sb = keep.tile([B, O], F32)
        nc.vector.tensor_tensor(out=out_sb[:], in0=out_ps[:], in1=bias_sb[:], op=ADD)
        nc.sync.dma_start(out=out, in_=out_sb[:])
